import numpy as np
import ml_dtypes


def mxq(x, axis, fmt="e4m3"):
    dtype, down = {"e4m3": (ml_dtypes.float8_e4m3fn, 7), "e5m2": (ml_dtypes.float8_e5m2, 14)}[fmt]
    v = np.moveaxis(np.asarray(x, np.float32).astype(ml_dtypes.bfloat16).astype(np.float64), axis, -1)
    blocks = v.reshape(v.shape[:-1] + (-1, 32))
    amax = np.abs(blocks).max(-1, keepdims=True)
    byte = np.maximum(np.where(amax > 0, np.frexp(amax)[1] - 1 + 127, 0) - down, 1)
    scale = np.exp2(byte - 127.0)
    codes = (blocks / scale).astype(np.float32).astype(dtype).astype(np.float64)
    return np.moveaxis((codes * scale).reshape(v.shape), -1, axis)


WIDE = False


def mx_kscale(k):
    if not WIDE:
        return np.ones(k)
    levels = np.array([10, -10, 5, -5, 0])
    a = np.random.permutation(np.resize(levels, k // 512 * 4)).reshape(k // 512, 4)
    idx = np.arange(k)
    return np.exp2(a[idx // 512, idx % 128 // 32])


BF16 = ml_dtypes.bfloat16


def bf(x):
    return np.asarray(x, np.float32).astype(BF16)


def f64(x):
    return np.asarray(x).astype(np.float64)


B, N, D, Q, HG, OG, HF, OF = 4, 64, 256, 512, 128, 512, 512, 256
K0 = 2 * D + Q
P = N * N


def setup_inputs():
    s = mx_kscale(K0)
    sx, sq = s[:D], s[2 * D:]
    sw = np.concatenate([sx, sx, sq])
    return {"x": bf(np.random.standard_normal((B, N, D)) * sx),
            "q": bf(np.random.standard_normal((B, Q)) * sq),
            "g_w0": bf(np.random.standard_normal((K0, HG)) / np.sqrt(K0) / sw[:, None]),
            "g_b0": bf(np.random.standard_normal(HG) * 0.3)}


def reference(x, q, g_w0, g_b0):
    x, q = f64(x), f64(q)
    xi = np.tile(x, (1, N, 1))
    xj = np.repeat(x, N, axis=1)
    qr = np.broadcast_to(q[:, None, :], (B, P, Q))
    pair = np.concatenate([xi, xj, qr], axis=2)
    return np.maximum((mxq(pair, 2, "e4m3") @ mxq(f64(g_w0), 0, "e4m3")) + f64(g_b0), 0.0)

@@ -1,0 +1,167 @@
+import concourse.mybir as mybir
+from concourse.masks import make_identity
+
+F32 = mybir.dt.float32
+BF16 = mybir.dt.bfloat16
+U32 = mybir.dt.uint32
+U8 = mybir.dt.uint8
+FP8X4 = mybir.dt.float8_e4m3fn_x4
+ADD = mybir.AluOpType.add
+MAX = mybir.AluOpType.max
+
+P = 128
+PACK = 4
+K_PASS = P * PACK
+B = 4
+N = 64
+D = 256
+H = 128
+ROWS = B * N
+ROW_TILES = ROWS // P
+HALF = D // PACK
+RUN = 8
+I_HI = N // RUN
+J_UNIT = P // I_HI
+UNITS = N // J_UNIT
+BANK = 512
+T_BANK = BANK // H
+
+W_U = 0
+W_V = 1
+W_Q = 2
+
+FLOPS = 2 * B * N * N * (2 * D + K_PASS) * H
+
+
+def tile_relationnetwork_pa_t_kernel(tc, x, q, g_w0, g_b0, out):
+    nc = tc.nc
+    with (
+        tc.tile_pool(name="keep", bufs=1) as keep,
+        tc.tile_pool(name="pairs", bufs=3) as pairs,
+        tc.tile_pool(name="stages", bufs=4) as stages,
+        tc.psum_pool(name="head_psum", bufs=1) as head_psum,
+        tc.psum_pool(name="turn_psum", bufs=5) as turn_psum,
+    ):
+        x_twice = keep.tile([P, ROW_TILES, 2, D], BF16)
+        x_rows = x.rearrange("b n k -> (b n) k").rearrange("(a r) k -> r a k", r=P)
+        nc.sync.dma_start(out=x_twice[:, :, 0, :], in_=x_rows)
+        nc.sync.dma_start(out=x_twice[:, :, 1, :], in_=x_rows)
+        w_raw = keep.tile([P, 2, PACK, H], BF16)
+        nc.scalar.dma_start(out=w_raw[:], in_=g_w0.rearrange("(c p t) h -> p c t h", c=2, t=PACK))
+        q_raw = keep.tile([P, B, PACK], BF16)
+        nc.sync.dma_start(out=q_raw[:], in_=q.rearrange("b (p t) -> p b t", t=PACK))
+        bias_raw = keep.tile([P, 1], BF16)
+        nc.scalar.dma_start(out=bias_raw[:], in_=g_b0.rearrange("(p o) -> p o", o=1))
+
+        identity = keep.tile([P, P], F32)
+        make_identity(nc, identity[:])
+
+        w_grouped = keep.tile([P, 3, H, PACK], BF16, align_bytes=64)
+        nc.vector.memset(w_grouped[HALF:P, W_U, :, :], 0.0)
+        nc.vector.memset(w_grouped[0:HALF, W_V, :, :], 0.0)
+        nc.vector.tensor_copy(
+            out=w_grouped[0:HALF, W_U, :, :], in_=w_raw[0:HALF, 0, :, :].rearrange("p t h -> p h t")
+        )
+        nc.vector.tensor_copy(
+            out=w_grouped[HALF:P, W_V, :, :], in_=w_raw[HALF:P, 0, :, :].rearrange("p t h -> p h t")
+        )
+        nc.scalar.copy(out=w_grouped[:, W_Q, :, :], in_=w_raw[:, 1, :, :].rearrange("p t h -> p h t"))
+        w_codes = keep.tile([P, 3, H], U32, align_bytes=64)
+        w_scales = keep.tile([P, 3, H], U8, align_bytes=64)
+        nc.vector.quantize_mx(
+            out=w_codes[:, W_U : W_V + 1, :].rearrange("p s h -> p (s h)").bitcast(FP8X4),
+            scales=w_scales[:, W_U : W_V + 1, :].rearrange("p s h -> p (s h)"),
+            in_=w_grouped[:, W_U : W_V + 1, :, :].rearrange("p s h t -> p (s h t)"),
+        )
+
+        q_grouped = keep.tile([P, B, N, PACK], BF16, align_bytes=64)
+        nc.vector.tensor_copy(
+            out=q_grouped[:], in_=q_raw[:].unsqueeze(2).to_broadcast([P, B, N, PACK])
+        )
+        nc.vector.quantize_mx(
+            out=w_codes[:, W_Q, :].bitcast(FP8X4),
+            scales=w_scales[:, W_Q, :],
+            in_=w_grouped[:, W_Q, :, :].rearrange("p h t -> p (h t)"),
+        )
+        q_codes = keep.tile([P, ROWS], U32, align_bytes=64)
+        q_scales = keep.tile([P, ROWS], U8, align_bytes=64)
+        nc.vector.quantize_mx(
+            out=q_codes[:].bitcast(FP8X4),
+            scales=q_scales[:],
+            in_=q_grouped[:].rearrange("p b n t -> p (b n t)"),
+        )
+
+        x_turned = head_psum.tile([P, 2, ROWS], F32)
+        for a in range(ROW_TILES):
+            words = x_twice[:, a, :, :].rearrange("r d k -> r (d k)").bitcast(F32)
+            words = words.rearrange("r (p u) -> r p u", u=2)
+            for u in range(2):
+                nc.tensor.transpose(x_turned[:, u, a * P : (a + 1) * P], words[:, :, u], identity[:])
+        x_grouped = keep.tile([P, ROWS, PACK], BF16, align_bytes=64)
+        nc.scalar.copy(
+            out=x_grouped[:].rearrange("p c t -> p (c t)").bitcast(F32).rearrange("p (c u) -> p c u", u=2),
+            in_=x_turned[:].rearrange("p u c -> p c u"),
+        )
+        x_codes = keep.tile([P, ROWS], U32, align_bytes=64)
+        x_scales = keep.tile([P, ROWS], U8, align_bytes=64)
+        nc.vector.quantize_mx(
+            out=x_codes[:].bitcast(FP8X4),
+            scales=x_scales[:],
+            in_=x_grouped[:].rearrange("p c t -> p (c t)"),
+        )
+
+        bias = keep.tile([P, 1], F32)
+        nc.vector.tensor_copy(out=bias[:], in_=bias_raw[:])
+
+        def mx_pass(acc, w_slot, codes, scales, start, stop):
+            nc.tensor.matmul_mx(
+                out=acc,
+                lhsT=w_codes[:, w_slot, :].bitcast(FP8X4),
+                lhsT_scale=w_scales[:, w_slot, :],
+                rhs=codes[:].bitcast(FP8X4),
+                rhs_scale=scales[:],
+                start=start,
+                stop=stop,
+            )
+
+        u_psum = head_psum.tile([P, BANK], F32)
+        v_psum = head_psum.tile([P, BANK], F32)
+        mx_pass(u_psum[:, 0:ROWS], W_U, x_codes, x_scales, True, True)
+        mx_pass(v_psum[:, 0:ROWS], W_V, x_codes, x_scales, True, False)
+        mx_pass(v_psum[:, 0:ROWS], W_Q, q_codes, q_scales, False, True)
+        u_sb = keep.tile([P, B, RUN, I_HI], F32)
+        nc.scalar.copy(
+            out=u_sb[:], in_=u_psum[:, 0:ROWS].rearrange("p (b i r) -> p b r i", b=B, r=RUN)
+        )
+        v_sb = keep.tile([P, ROWS], F32)
+        nc.vector.tensor_scalar(
+            out=v_sb[:], in0=v_psum[:, 0:ROWS], scalar1=bias[:, 0:1], scalar2=None, op0=ADD
+        )
+
+        out_units = out.rearrange("b (g m r) h -> (b g) m (r h)", g=UNITS, m=P, r=RUN)
+        for b in range(B):
+            for g in range(UNITS):
+                first_j = b * N + g * J_UNIT
+                pair_relu = pairs.tile([P, RUN, J_UNIT, I_HI], F32)
+                for j in range(J_UNIT):
+                    nc.vector.tensor_scalar(
+                        out=pair_relu[:, :, j, :],
+                        in0=u_sb[:, b, :, :],
+                        scalar1=v_sb[:, first_j + j : first_j + j + 1],
+                        scalar2=0.0,
+                        op0=ADD,
+                        op1=MAX,
+                    )
+                stage = stages.tile([P, RUN, H], F32)
+                for r0 in range(0, RUN, T_BANK):
+                    turned = turn_psum.tile([P, T_BANK, H], F32)
+                    for r in range(T_BANK):
+                        nc.tensor.transpose(
+                            turned[:, r, :],
+                            pair_relu[:, r0 + r, :, :].rearrange("p j i -> p (j i)"),
+                            identity[:],
+                        )
+                    nc.scalar.copy(out=stage[:, r0 : r0 + T_BANK, :], in_=turned[:])
+                nc.sync.dma_start(
+                    out=out_units[b * UNITS + g], in_=stage[:].rearrange("m r h -> m (r h)")
+                )

@@ -16,9 +16,10 @@ B = 4
 N = 64
 D = 256
 H = 128
-ROWS = B * N
-ROW_TILES = ROWS // P
+ROW_TILES = B * N // P
+B_TILE = P // N
 HALF = D // PACK
+Q_COPIES = 16
 RUN = 8
 I_HI = N // RUN
 J_UNIT = P // I_HI
@@ -28,7 +29,7 @@ T_BANK = BANK // H
 
 W_U = 0
 W_V = 1
-W_Q = 2
+W_C = 2
 
 FLOPS = 2 * B * N * N * (2 * D + K_PASS) * H
 
@@ -37,131 +38,168 @@ def tile_relationnetwork_pa_t_kernel(tc, x, q, g_w0, g_b0, out):
     nc = tc.nc
     with (
         tc.tile_pool(name="keep", bufs=1) as keep,
-        tc.tile_pool(name="pairs", bufs=3) as pairs,
+        tc.tile_pool(name="pairs", bufs=4) as pairs,
         tc.tile_pool(name="stages", bufs=4) as stages,
-        tc.psum_pool(name="head_psum", bufs=1) as head_psum,
-        tc.psum_pool(name="turn_psum", bufs=5) as turn_psum,
+        tc.psum_pool(name="fact_psum", bufs=2) as fact_psum,
+        tc.psum_pool(name="sum_psum", bufs=1) as sum_psum,
+        tc.psum_pool(name="turn_psum", bufs=4) as turn_psum,
     ):
         x_twice = keep.tile([P, ROW_TILES, 2, D], BF16)
-        x_rows = x.rearrange("b n k -> (b n) k").rearrange("(a r) k -> r a k", r=P)
-        nc.sync.dma_start(out=x_twice[:, :, 0, :], in_=x_rows)
-        nc.sync.dma_start(out=x_twice[:, :, 1, :], in_=x_rows)
+        x_tiles = x.rearrange("b n k -> (b n) k").rearrange("(a r) k -> a r k", r=P)
+
+        def load_facts(a):
+            nc.sync.dma_start(out=x_twice[:, a, 0, :], in_=x_tiles[a])
+            nc.scalar.dma_start(out=x_twice[:, a, 1, :], in_=x_tiles[a])
+
+        load_facts(0)
         w_raw = keep.tile([P, 2, PACK, H], BF16)
-        nc.scalar.dma_start(out=w_raw[:], in_=g_w0.rearrange("(c p t) h -> p c t h", c=2, t=PACK))
+        nc.sync.dma_start(out=w_raw[:], in_=g_w0.rearrange("(c p t) h -> p c t h", c=2, t=PACK))
         q_raw = keep.tile([P, B, PACK], BF16)
-        nc.sync.dma_start(out=q_raw[:], in_=q.rearrange("b (p t) -> p b t", t=PACK))
+        nc.scalar.dma_start(out=q_raw[:], in_=q.rearrange("b (p t) -> p b t", t=PACK))
         bias_raw = keep.tile([P, 1], BF16)
         nc.scalar.dma_start(out=bias_raw[:], in_=g_b0.rearrange("(p o) -> p o", o=1))
+        load_facts(1)
 
         identity = keep.tile([P, P], F32)
         make_identity(nc, identity[:])
 
+        x_grouped = keep.tile([P, ROW_TILES, P, PACK], BF16, align_bytes=64)
+        x_codes = keep.tile([P, ROW_TILES, P], U32, align_bytes=64)
+        x_scales = keep.tile([P, ROW_TILES, P], U8, align_bytes=64)
+
+        def turn_facts(a):
+            words = x_twice[:, a, :, :].rearrange("r d k -> r (d k)").bitcast(F32)
+            words = words.rearrange("r (p u) -> r p u", u=2)
+            x_turned = fact_psum.tile([P, 2, P], F32, tag="head")
+            for u in range(2):
+                nc.tensor.transpose(x_turned[:, u, :], words[:, :, u], identity[:])
+            nc.scalar.copy(
+                out=x_grouped[:, a, :, :]
+                .rearrange("p c t -> p (c t)")
+                .bitcast(F32)
+                .rearrange("p (c u) -> p c u", u=2),
+                in_=x_turned[:].rearrange("p u c -> p c u"),
+            )
+
+        def quantise_facts(a):
+            nc.vector.quantize_mx(
+                out=x_codes[:, a, :].bitcast(FP8X4),
+                scales=x_scales[:, a, :],
+                in_=x_grouped[:, a, :, :].rearrange("p c t -> p (c t)"),
+            )
+
         w_grouped = keep.tile([P, 3, H, PACK], BF16, align_bytes=64)
+        w_codes = keep.tile([P, 3, H], U32, align_bytes=64)
+        w_scales = keep.tile([P, 3, H], U8, align_bytes=64)
         nc.vector.memset(w_grouped[HALF:P, W_U, :, :], 0.0)
         nc.vector.memset(w_grouped[0:HALF, W_V, :, :], 0.0)
+
+        turn_facts(0)
         nc.vector.tensor_copy(
             out=w_grouped[0:HALF, W_U, :, :], in_=w_raw[0:HALF, 0, :, :].rearrange("p t h -> p h t")
         )
         nc.vector.tensor_copy(
             out=w_grouped[HALF:P, W_V, :, :], in_=w_raw[HALF:P, 0, :, :].rearrange("p t h -> p h t")
         )
-        nc.scalar.copy(out=w_grouped[:, W_Q, :, :], in_=w_raw[:, 1, :, :].rearrange("p t h -> p h t"))
-        w_codes = keep.tile([P, 3, H], U32, align_bytes=64)
-        w_scales = keep.tile([P, 3, H], U8, align_bytes=64)
+        nc.scalar.copy(out=w_grouped[:, W_C, :, :], in_=w_raw[:, 1, :, :].rearrange("p t h -> p h t"))
+        turn_facts(1)
         nc.vector.quantize_mx(
             out=w_codes[:, W_U : W_V + 1, :].rearrange("p s h -> p (s h)").bitcast(FP8X4),
             scales=w_scales[:, W_U : W_V + 1, :].rearrange("p s h -> p (s h)"),
             in_=w_grouped[:, W_U : W_V + 1, :, :].rearrange("p s h t -> p (s h t)"),
         )
+        quantise_facts(0)
 
-        q_grouped = keep.tile([P, B, N, PACK], BF16, align_bytes=64)
-        nc.vector.tensor_copy(
-            out=q_grouped[:], in_=q_raw[:].unsqueeze(2).to_broadcast([P, B, N, PACK])
-        )
-        nc.vector.quantize_mx(
-            out=w_codes[:, W_Q, :].bitcast(FP8X4),
-            scales=w_scales[:, W_Q, :],
-            in_=w_grouped[:, W_Q, :, :].rearrange("p h t -> p (h t)"),
-        )
-        q_codes = keep.tile([P, ROWS], U32, align_bytes=64)
-        q_scales = keep.tile([P, ROWS], U8, align_bytes=64)
-        nc.vector.quantize_mx(
-            out=q_codes[:].bitcast(FP8X4),
-            scales=q_scales[:],
-            in_=q_grouped[:].rearrange("p b n t -> p (b n t)"),
-        )
-
-        x_turned = head_psum.tile([P, 2, ROWS], F32)
-        for a in range(ROW_TILES):
-            words = x_twice[:, a, :, :].rearrange("r d k -> r (d k)").bitcast(F32)
-            words = words.rearrange("r (p u) -> r p u", u=2)
-            for u in range(2):
-                nc.tensor.transpose(x_turned[:, u, a * P : (a + 1) * P], words[:, :, u], identity[:])
-        x_grouped = keep.tile([P, ROWS, PACK], BF16, align_bytes=64)
-        nc.scalar.copy(
-            out=x_grouped[:].rearrange("p c t -> p (c t)").bitcast(F32).rearrange("p (c u) -> p c u", u=2),
-            in_=x_turned[:].rearrange("p u c -> p c u"),
-        )
-        x_codes = keep.tile([P, ROWS], U32, align_bytes=64)
-        x_scales = keep.tile([P, ROWS], U8, align_bytes=64)
-        nc.vector.quantize_mx(
-            out=x_codes[:].bitcast(FP8X4),
-            scales=x_scales[:],
-            in_=x_grouped[:].rearrange("p c t -> p (c t)"),
-        )
-
-        bias = keep.tile([P, 1], F32)
-        nc.vector.tensor_copy(out=bias[:], in_=bias_raw[:])
-
-        def mx_pass(acc, w_slot, codes, scales, start, stop):
+        def mx_pass(acc, w_slot, codes, scales):
             nc.tensor.matmul_mx(
                 out=acc,
                 lhsT=w_codes[:, w_slot, :].bitcast(FP8X4),
                 lhsT_scale=w_scales[:, w_slot, :],
-                rhs=codes[:].bitcast(FP8X4),
-                rhs_scale=scales[:],
-                start=start,
-                stop=stop,
+                rhs=codes.bitcast(FP8X4),
+                rhs_scale=scales,
+                start=True,
+                stop=True,
             )
 
-        u_psum = head_psum.tile([P, BANK], F32)
-        v_psum = head_psum.tile([P, BANK], F32)
-        mx_pass(u_psum[:, 0:ROWS], W_U, x_codes, x_scales, True, True)
-        mx_pass(v_psum[:, 0:ROWS], W_V, x_codes, x_scales, True, False)
-        mx_pass(v_psum[:, 0:ROWS], W_Q, q_codes, q_scales, False, True)
         u_sb = keep.tile([P, B, RUN, I_HI], F32)
-        nc.scalar.copy(
-            out=u_sb[:], in_=u_psum[:, 0:ROWS].rearrange("p (b i r) -> p b r i", b=B, r=RUN)
-        )
-        v_sb = keep.tile([P, ROWS], F32)
-        nc.vector.tensor_scalar(
-            out=v_sb[:], in0=v_psum[:, 0:ROWS], scalar1=bias[:, 0:1], scalar2=None, op0=ADD
-        )
+        v_sb = keep.tile([P, B, N], F32)
+        c_sb = keep.tile([P, B], F32)
 
-        out_units = out.rearrange("b (g m r) h -> (b g) m (r h)", g=UNITS, m=P, r=RUN)
-        for b in range(B):
-            for g in range(UNITS):
-                first_j = b * N + g * J_UNIT
-                pair_relu = pairs.tile([P, RUN, J_UNIT, I_HI], F32)
-                for j in range(J_UNIT):
-                    nc.vector.tensor_scalar(
-                        out=pair_relu[:, :, j, :],
-                        in0=u_sb[:, b, :, :],
-                        scalar1=v_sb[:, first_j + j : first_j + j + 1],
-                        scalar2=0.0,
-                        op0=ADD,
-                        op1=MAX,
-                    )
-                stage = stages.tile([P, RUN, H], F32)
-                for r0 in range(0, RUN, T_BANK):
-                    turned = turn_psum.tile([P, T_BANK, H], F32)
-                    for r in range(T_BANK):
-                        nc.tensor.transpose(
-                            turned[:, r, :],
-                            pair_relu[:, r0 + r, :, :].rearrange("p j i -> p (j i)"),
-                            identity[:],
-                        )
-                    nc.scalar.copy(out=stage[:, r0 : r0 + T_BANK, :], in_=turned[:])
-                nc.sync.dma_start(
-                    out=out_units[b * UNITS + g], in_=stage[:].rearrange("m r h -> m (r h)")
+        def multiply_facts(a):
+            u_psum = sum_psum.tile([P, P], F32)
+            v_psum = sum_psum.tile([P, B_TILE, N], F32)
+            mx_pass(u_psum[:], W_U, x_codes[:, a, :], x_scales[:, a, :])
+            mx_pass(v_psum[:].rearrange("p s j -> p (s j)"), W_V, x_codes[:, a, :], x_scales[:, a, :])
+            nc.scalar.copy(
+                out=u_sb[:, a * B_TILE : (a + 1) * B_TILE, :, :],
+                in_=u_psum[:].rearrange("p (s i r) -> p s r i", s=B_TILE, r=RUN),
+            )
+            return v_psum
+
+        def finish_v(a, v_psum):
+            for s in range(B_TILE):
+                b = a * B_TILE + s
+                nc.vector.tensor_scalar(
+                    out=v_sb[:, b, :], in0=v_psum[:, s, :], scalar1=c_sb[:, b : b + 1], scalar2=None, op0=ADD
                 )
+
+        v_psum_0 = multiply_facts(0)
+
+        q_grouped = keep.tile([P, B, Q_COPIES, PACK], BF16, align_bytes=64)
+        nc.vector.tensor_copy(
+            out=q_grouped[:], in_=q_raw[:].unsqueeze(2).to_broadcast([P, B, Q_COPIES, PACK])
+        )
+        nc.vector.quantize_mx(
+            out=w_codes[:, W_C, :].bitcast(FP8X4),
+            scales=w_scales[:, W_C, :],
+            in_=w_grouped[:, W_C, :, :].rearrange("p h t -> p (h t)"),
+        )
+        q_codes = keep.tile([P, B * Q_COPIES], U32, align_bytes=64)
+        q_scales = keep.tile([P, B * Q_COPIES], U8, align_bytes=64)
+        nc.vector.quantize_mx(
+            out=q_codes[:].bitcast(FP8X4),
+            scales=q_scales[:],
+            in_=q_grouped[:].rearrange("p b s t -> p (b s t)"),
+        )
+        bias = keep.tile([P, 1], F32)
+        nc.vector.tensor_copy(out=bias[:], in_=bias_raw[:])
+        c_psum = fact_psum.tile([P, B, Q_COPIES], F32, tag="head")
+        mx_pass(c_psum[:].rearrange("p b s -> p (b s)"), W_C, q_codes[:], q_scales[:])
+        quantise_facts(1)
+        nc.vector.tensor_scalar(
+            out=c_sb[:], in0=c_psum[:, :, 0], scalar1=bias[:, 0:1], scalar2=None, op0=ADD
+        )
+        finish_v(0, v_psum_0)
+        finish_v(1, multiply_facts(1))
+
+        out_units = out.rearrange("b (g m r) h -> (b g) m r h", g=UNITS, m=P, r=RUN)
+        for unit in range(B * UNITS):
+            b, g = divmod(unit, UNITS)
+            pair_relu = pairs.tile([P, RUN, J_UNIT, I_HI], F32)
+            for j_lo in range(J_UNIT):
+                j = g * J_UNIT + j_lo
+                nc.vector.tensor_scalar(
+                    out=pair_relu[:, :, j_lo, :],
+                    in0=u_sb[:, b, :, :],
+                    scalar1=v_sb[:, b, j : j + 1],
+                    scalar2=0.0,
+                    op0=ADD,
+                    op1=MAX,
+                )
+            stage = stages.tile([P, RUN, H], F32)
+            stored_at_once = T_BANK if unit == B * UNITS - 1 else RUN
+            for r0 in range(0, RUN, T_BANK):
+                turned = turn_psum.tile([P, T_BANK, H], F32)
+                for r in range(T_BANK):
+                    nc.tensor.transpose(
+                        turned[:, r, :],
+                        pair_relu[:, r0 + r, :, :].rearrange("p j i -> p (j i)"),
+                        identity[:],
+                    )
+                nc.scalar.copy(out=stage[:, r0 : r0 + T_BANK, :], in_=turned[:])
+                r_end = r0 + T_BANK
+                if r_end % stored_at_once == 0:
+                    nc.sync.dma_start(
+                        out=out_units[unit, :, r_end - stored_at_once : r_end, :],
+                        in_=stage[:, r_end - stored_at_once : r_end, :],
+                    )

@@ -170,10 +170,11 @@ def tile_relationnetwork_pa_t_kernel(tc, x, q, g_w0, g_b0, out):
             out=c_sb[:], in0=c_psum[:, :, 0], scalar1=bias[:, 0:1], scalar2=None, op0=ADD
         )
         finish_v(0, v_psum_0)
-        finish_v(1, multiply_facts(1))
 
         out_units = out.rearrange("b (g m r) h -> (b g) m r h", g=UNITS, m=P, r=RUN)
-        for unit in range(B * UNITS):
+        last_unit = B * UNITS - 1
+
+        def add_pairs(unit):
             b, g = divmod(unit, UNITS)
             pair_relu = pairs.tile([P, RUN, J_UNIT, I_HI], F32)
             for j_lo in range(J_UNIT):
@@ -186,8 +187,11 @@ def tile_relationnetwork_pa_t_kernel(tc, x, q, g_w0, g_b0, out):
                     op0=ADD,
                     op1=MAX,
                 )
+            return pair_relu
+
+        def turn_and_store(unit, pair_relu):
             stage = stages.tile([P, RUN, H], F32)
-            stored_at_once = T_BANK if unit == B * UNITS - 1 else RUN
+            stored_at_once = T_BANK if unit == last_unit else RUN
             for r0 in range(0, RUN, T_BANK):
                 turned = turn_psum.tile([P, T_BANK, H], F32)
                 for r in range(T_BANK):
@@ -197,9 +201,24 @@ def tile_relationnetwork_pa_t_kernel(tc, x, q, g_w0, g_b0, out):
                         identity[:],
                     )
                 nc.scalar.copy(out=stage[:, r0 : r0 + T_BANK, :], in_=turned[:])
+                if r0 == 0:
+                    mx_pass(warm_psum[:], W_U, warm_codes[:], warm_scales[:])
                 r_end = r0 + T_BANK
                 if r_end % stored_at_once == 0:
                     nc.sync.dma_start(
                         out=out_units[unit, :, r_end - stored_at_once : r_end, :],
                         in_=stage[:, r_end - stored_at_once : r_end, :],
                     )
+
+        warm_zeros = keep.tile([P, BANK * PACK], BF16, align_bytes=64)
+        warm_codes = keep.tile([P, BANK], U32, align_bytes=64)
+        warm_scales = keep.tile([P, BANK], U8, align_bytes=64)
+        nc.vector.memset(warm_zeros[:], 0.0)
+        nc.vector.quantize_mx(out=warm_codes[:].bitcast(FP8X4), scales=warm_scales[:], in_=warm_zeros[:])
+        warm_psum = fact_psum.tile([P, BANK], F32, tag="head")
+
+        first_pairs = add_pairs(0)
+        finish_v(1, multiply_facts(1))
+        turn_and_store(0, first_pairs)
+        for unit in range(1, B * UNITS):
+            turn_and_store(unit, add_pairs(unit))

@@ -39,7 +39,7 @@ def tile_relationnetwork_pa_t_kernel(tc, x, q, g_w0, g_b0, out):
     with (
         tc.tile_pool(name="keep", bufs=1) as keep,
         tc.tile_pool(name="pairs", bufs=4) as pairs,
-        tc.tile_pool(name="stages", bufs=4) as stages,
+        tc.tile_pool(name="stages", bufs=8) as stages,
         tc.psum_pool(name="fact_psum", bufs=2) as fact_psum,
         tc.psum_pool(name="sum_psum", bufs=1) as sum_psum,
         tc.psum_pool(name="turn_psum", bufs=4) as turn_psum,
@@ -48,16 +48,18 @@ def tile_relationnetwork_pa_t_kernel(tc, x, q, g_w0, g_b0, out):
         x_tiles = x.rearrange("b n k -> (b n) k").rearrange("(a r) k -> a r k", r=P)
 
         def load_facts(a):
-            nc.sync.dma_start(out=x_twice[:, a, 0, :], in_=x_tiles[a])
-            nc.scalar.dma_start(out=x_twice[:, a, 1, :], in_=x_tiles[a])
+            for twin in range(2):
+                nc.sync.dma_start(out=x_twice[:, a, twin, :], in_=x_tiles[a])
 
-        load_facts(0)
         w_raw = keep.tile([P, 2, PACK, H], BF16)
-        nc.sync.dma_start(out=w_raw[:], in_=g_w0.rearrange("(c p t) h -> p c t h", c=2, t=PACK))
+        w_halves = g_w0.rearrange("(c p t) h -> c p t h", c=2, t=PACK)
         q_raw = keep.tile([P, B, PACK], BF16)
-        nc.scalar.dma_start(out=q_raw[:], in_=q.rearrange("b (p t) -> p b t", t=PACK))
         bias_raw = keep.tile([P, 1], BF16)
-        nc.scalar.dma_start(out=bias_raw[:], in_=g_b0.rearrange("(p o) -> p o", o=1))
+        load_facts(0)
+        nc.sync.dma_start(out=w_raw[:, 0, :, :], in_=w_halves[0])
+        nc.sync.dma_start(out=w_raw[:, 1, :, :], in_=w_halves[1])
+        nc.sync.dma_start(out=q_raw[:], in_=q.rearrange("b (p t) -> p b t", t=PACK))
+        nc.sync.dma_start(out=bias_raw[:], in_=g_b0.rearrange("(p o) -> p o", o=1))
         load_facts(1)
 
         identity = keep.tile([P, P], F32)
@@ -170,11 +172,10 @@ def tile_relationnetwork_pa_t_kernel(tc, x, q, g_w0, g_b0, out):
             out=c_sb[:], in0=c_psum[:, :, 0], scalar1=bias[:, 0:1], scalar2=None, op0=ADD
         )
         finish_v(0, v_psum_0)
+        finish_v(1, multiply_facts(1))
 
         out_units = out.rearrange("b (g m r) h -> (b g) m r h", g=UNITS, m=P, r=RUN)
-        last_unit = B * UNITS - 1
-
-        def add_pairs(unit):
+        for unit in range(B * UNITS):
             b, g = divmod(unit, UNITS)
             pair_relu = pairs.tile([P, RUN, J_UNIT, I_HI], F32)
             for j_lo in range(J_UNIT):
@@ -187,11 +188,8 @@ def tile_relationnetwork_pa_t_kernel(tc, x, q, g_w0, g_b0, out):
                     op0=ADD,
                     op1=MAX,
                 )
-            return pair_relu
-
-        def turn_and_store(unit, pair_relu):
             stage = stages.tile([P, RUN, H], F32)
-            stored_at_once = T_BANK if unit == last_unit else RUN
+            stored_at_once = T_BANK if unit == B * UNITS - 1 else RUN
             for r0 in range(0, RUN, T_BANK):
                 turned = turn_psum.tile([P, T_BANK, H], F32)
                 for r in range(T_BANK):
@@ -201,24 +199,9 @@ def tile_relationnetwork_pa_t_kernel(tc, x, q, g_w0, g_b0, out):
                         identity[:],
                     )
                 nc.scalar.copy(out=stage[:, r0 : r0 + T_BANK, :], in_=turned[:])
-                if r0 == 0:
-                    mx_pass(warm_psum[:], W_U, warm_codes[:], warm_scales[:])
                 r_end = r0 + T_BANK
                 if r_end % stored_at_once == 0:
                     nc.sync.dma_start(
                         out=out_units[unit, :, r_end - stored_at_once : r_end, :],
                         in_=stage[:, r_end - stored_at_once : r_end, :],
                     )
-
-        warm_zeros = keep.tile([P, BANK * PACK], BF16, align_bytes=64)
-        warm_codes = keep.tile([P, BANK], U32, align_bytes=64)
-        warm_scales = keep.tile([P, BANK], U8, align_bytes=64)
-        nc.vector.memset(warm_zeros[:], 0.0)
-        nc.vector.quantize_mx(out=warm_codes[:].bitcast(FP8X4), scales=warm_scales[:], in_=warm_zeros[:])
-        warm_psum = fact_psum.tile([P, BANK], F32, tag="head")
-
-        first_pairs = add_pairs(0)
-        finish_v(1, multiply_facts(1))
-        turn_and_store(0, first_pairs)
-        for unit in range(1, B * UNITS):
-            turn_and_store(unit, add_pairs(unit))

@@ -8,6 +8,8 @@ U8 = mybir.dt.uint8
 FP8X4 = mybir.dt.float8_e4m3fn_x4
 ADD = mybir.AluOpType.add
 MAX = mybir.AluOpType.max
+RELU = mybir.ActivationFunctionType.Relu
+IDENTITY = mybir.ActivationFunctionType.Identity
 
 P = 128
 PACK = 4
@@ -16,20 +18,18 @@ B = 4
 N = 64
 D = 256
 H = 128
-ROW_TILES = B * N // P
+TILES = B * N // P
 B_TILE = P // N
 HALF = D // PACK
-Q_COPIES = 16
 RUN = 8
 I_HI = N // RUN
 J_UNIT = P // I_HI
 UNITS = N // J_UNIT
-BANK = 512
-T_BANK = BANK // H
+T_BANK = 4
+RAMP = 2
 
-W_U = 0
-W_V = 1
-W_C = 2
+FOR_U = 0
+FOR_V = 1
 
 FLOPS = 2 * B * N * N * (2 * D + K_PASS) * H
 
@@ -40,11 +40,11 @@ def tile_relationnetwork_pa_t_kernel(tc, x, q, g_w0, g_b0, out):
         tc.tile_pool(name="keep", bufs=1) as keep,
         tc.tile_pool(name="pairs", bufs=4) as pairs,
         tc.tile_pool(name="stages", bufs=8) as stages,
-        tc.psum_pool(name="fact_psum", bufs=2) as fact_psum,
-        tc.psum_pool(name="sum_psum", bufs=1) as sum_psum,
-        tc.psum_pool(name="turn_psum", bufs=4) as turn_psum,
+        tc.psum_pool(name="head_psum", bufs=1) as head_psum,
+        tc.psum_pool(name="turn_psum", bufs=5) as turn_psum,
+        tc.manual_schedule(),
     ):
-        x_twice = keep.tile([P, ROW_TILES, 2, D], BF16)
+        x_twice = keep.tile([P, TILES, 2, D], BF16)
         x_tiles = x.rearrange("b n k -> (b n) k").rearrange("(a r) k -> a r k", r=P)
 
         def load_facts(a):
@@ -52,156 +52,206 @@ def tile_relationnetwork_pa_t_kernel(tc, x, q, g_w0, g_b0, out):
                 nc.sync.dma_start(out=x_twice[:, a, twin, :], in_=x_tiles[a])
 
         w_raw = keep.tile([P, 2, PACK, H], BF16)
-        w_halves = g_w0.rearrange("(c p t) h -> c p t h", c=2, t=PACK)
+        w_quarters = g_w0.rearrange("(c p t) h -> c p t h", c=4, t=PACK)
         q_raw = keep.tile([P, B, PACK], BF16)
-        bias_raw = keep.tile([P, 1], BF16)
+        bias = keep.tile([P, 1], BF16)
+        nc.scalar.dma_start(out=q_raw[:], in_=q.rearrange("b (p t) -> p b t", t=PACK))
         load_facts(0)
-        nc.sync.dma_start(out=w_raw[:, 0, :, :], in_=w_halves[0])
-        nc.sync.dma_start(out=w_raw[:, 1, :, :], in_=w_halves[1])
-        nc.sync.dma_start(out=q_raw[:], in_=q.rearrange("b (p t) -> p b t", t=PACK))
-        nc.sync.dma_start(out=bias_raw[:], in_=g_b0.rearrange("(p o) -> p o", o=1))
+        nc.sync.dma_start(out=w_raw[0:HALF, FOR_U, :, :], in_=w_quarters[0])
+        nc.sync.dma_start(out=w_raw[HALF:P, FOR_U, :, :], in_=w_quarters[3])
+        nc.sync.dma_start(out=w_raw[0:HALF, FOR_V, :, :], in_=w_quarters[2])
+        nc.sync.dma_start(out=w_raw[HALF:P, FOR_V, :, :], in_=w_quarters[1])
+        nc.sync.dma_start(out=bias[:], in_=g_b0.rearrange("(p o) -> p o", o=1))
         load_facts(1)
 
         identity = keep.tile([P, P], F32)
         make_identity(nc, identity[:])
 
-        x_grouped = keep.tile([P, ROW_TILES, P, PACK], BF16, align_bytes=64)
-        x_codes = keep.tile([P, ROW_TILES, P], U32, align_bytes=64)
-        x_scales = keep.tile([P, ROW_TILES, P], U8, align_bytes=64)
+        x_grouped = keep.tile([P, TILES, 2, P, PACK], BF16, align_bytes=64)
+        x_codes = keep.tile([P, TILES, 2, P], U32, align_bytes=64)
+        x_scales = keep.tile([P, TILES, 2, P], U8, align_bytes=64)
+        w_grouped = keep.tile([P, 2, H, PACK], BF16, align_bytes=64)
+        w_codes = keep.tile([P, 2, H], U32, align_bytes=64)
+        w_scales = keep.tile([P, 2, H], U8, align_bytes=64)
+
+        def words(rows):
+            return rows.rearrange("p c t -> p (c t)").bitcast(F32)
 
         def turn_facts(a):
-            words = x_twice[:, a, :, :].rearrange("r d k -> r (d k)").bitcast(F32)
-            words = words.rearrange("r (p u) -> r p u", u=2)
-            x_turned = fact_psum.tile([P, 2, P], F32, tag="head")
+            pair_words = x_twice[:, a, :, :].rearrange("r d k -> r (d k)").bitcast(F32)
+            pair_words = pair_words.rearrange("r (p u) -> r p u", u=2)
+            x_turned = head_psum.tile([P, 2, P], F32)
             for u in range(2):
-                nc.tensor.transpose(x_turned[:, u, :], words[:, :, u], identity[:])
-            nc.scalar.copy(
-                out=x_grouped[:, a, :, :]
-                .rearrange("p c t -> p (c t)")
-                .bitcast(F32)
-                .rearrange("p (c u) -> p c u", u=2),
-                in_=x_turned[:].rearrange("p u c -> p c u"),
-            )
+                nc.tensor.transpose(x_turned[:, u, :], pair_words[:, :, u], identity[:])
+            for use, lo in ((FOR_U, 0), (FOR_V, HALF)):
+                nc.scalar.copy(
+                    out=words(x_grouped[lo : lo + HALF, a, use, :, :]).rearrange("p (c u) -> p c u", u=2),
+                    in_=x_turned[lo : lo + HALF, :, :].rearrange("p u c -> p c u"),
+                )
 
         def quantise_facts(a):
             nc.vector.quantize_mx(
-                out=x_codes[:, a, :].bitcast(FP8X4),
-                scales=x_scales[:, a, :],
-                in_=x_grouped[:, a, :, :].rearrange("p c t -> p (c t)"),
+                out=x_codes[:, a, :, :].rearrange("p v c -> p (v c)").bitcast(FP8X4),
+                scales=x_scales[:, a, :, :].rearrange("p v c -> p (v c)"),
+                in_=x_grouped[:, a, :, :, :].rearrange("p v c t -> p (v c t)"),
             )
 
-        w_grouped = keep.tile([P, 3, H, PACK], BF16, align_bytes=64)
-        w_codes = keep.tile([P, 3, H], U32, align_bytes=64)
-        w_scales = keep.tile([P, 3, H], U8, align_bytes=64)
-        nc.vector.memset(w_grouped[HALF:P, W_U, :, :], 0.0)
-        nc.vector.memset(w_grouped[0:HALF, W_V, :, :], 0.0)
+        def group_weights(use):
+            nc.vector.tensor_copy(out=w_grouped[:, use, :, :], in_=w_raw[:, use, :, :].rearrange("p t h -> p h t"))
 
-        turn_facts(0)
-        nc.vector.tensor_copy(
-            out=w_grouped[0:HALF, W_U, :, :], in_=w_raw[0:HALF, 0, :, :].rearrange("p t h -> p h t")
-        )
-        nc.vector.tensor_copy(
-            out=w_grouped[HALF:P, W_V, :, :], in_=w_raw[HALF:P, 0, :, :].rearrange("p t h -> p h t")
-        )
-        nc.scalar.copy(out=w_grouped[:, W_C, :, :], in_=w_raw[:, 1, :, :].rearrange("p t h -> p h t"))
-        turn_facts(1)
-        nc.vector.quantize_mx(
-            out=w_codes[:, W_U : W_V + 1, :].rearrange("p s h -> p (s h)").bitcast(FP8X4),
-            scales=w_scales[:, W_U : W_V + 1, :].rearrange("p s h -> p (s h)"),
-            in_=w_grouped[:, W_U : W_V + 1, :, :].rearrange("p s h t -> p (s h t)"),
-        )
-        quantise_facts(0)
+        def quantise_weights():
+            nc.vector.quantize_mx(
+                out=w_codes[:].rearrange("p v h -> p (v h)").bitcast(FP8X4),
+                scales=w_scales[:].rearrange("p v h -> p (v h)"),
+                in_=w_grouped[:].rearrange("p v h t -> p (v h t)"),
+            )
 
-        def mx_pass(acc, w_slot, codes, scales):
+        def spread_questions(a):
+            for use, lo in ((FOR_V, 0), (FOR_U, HALF)):
+                nc.vector.tensor_copy(
+                    out=words(x_grouped[lo : lo + HALF, a, use, :, :]).rearrange("p (s n u) -> p s n u", s=B_TILE, u=2),
+                    in_=words(q_raw[lo : lo + HALF, a * B_TILE : (a + 1) * B_TILE, :])
+                    .rearrange("p (s u) -> p s u", u=2)
+                    .unsqueeze(2)
+                    .to_broadcast([HALF, B_TILE, N, 2]),
+                )
+
+        u_sb = keep.tile([P, B, RUN, I_HI], F32)
+        v_sb = keep.tile([P, B, N], F32)
+
+        def mx_pass(acc, a, use):
             nc.tensor.matmul_mx(
                 out=acc,
-                lhsT=w_codes[:, w_slot, :].bitcast(FP8X4),
-                lhsT_scale=w_scales[:, w_slot, :],
-                rhs=codes.bitcast(FP8X4),
-                rhs_scale=scales,
+                lhsT=w_codes[:, use, :].bitcast(FP8X4),
+                lhsT_scale=w_scales[:, use, :],
+                rhs=x_codes[:, a, use, :].bitcast(FP8X4),
+                rhs_scale=x_scales[:, a, use, :],
                 start=True,
                 stop=True,
             )
 
-        u_sb = keep.tile([P, B, RUN, I_HI], F32)
-        v_sb = keep.tile([P, B, N], F32)
-        c_sb = keep.tile([P, B], F32)
-
-        def multiply_facts(a):
-            u_psum = sum_psum.tile([P, P], F32)
-            v_psum = sum_psum.tile([P, B_TILE, N], F32)
-            mx_pass(u_psum[:], W_U, x_codes[:, a, :], x_scales[:, a, :])
-            mx_pass(v_psum[:].rearrange("p s j -> p (s j)"), W_V, x_codes[:, a, :], x_scales[:, a, :])
-            nc.scalar.copy(
+        def multiply(a):
+            u_psum = head_psum.tile([P, P], F32)
+            v_psum = head_psum.tile([P, B_TILE, N], F32)
+            mx_pass(u_psum[:], a, FOR_U)
+            mx_pass(v_psum[:].rearrange("p s j -> p (s j)"), a, FOR_V)
+            nc.scalar.activation(
                 out=u_sb[:, a * B_TILE : (a + 1) * B_TILE, :, :],
                 in_=u_psum[:].rearrange("p (s i r) -> p s r i", s=B_TILE, r=RUN),
+                func=IDENTITY,
+                bias=bias[:, 0:1],
             )
             return v_psum
 
         def finish_v(a, v_psum):
-            for s in range(B_TILE):
-                b = a * B_TILE + s
-                nc.vector.tensor_scalar(
-                    out=v_sb[:, b, :], in0=v_psum[:, s, :], scalar1=c_sb[:, b : b + 1], scalar2=None, op0=ADD
-                )
+            nc.vector.tensor_copy(out=v_sb[:, a * B_TILE : (a + 1) * B_TILE, :], in_=v_psum[:])
 
-        v_psum_0 = multiply_facts(0)
-
-        q_grouped = keep.tile([P, B, Q_COPIES, PACK], BF16, align_bytes=64)
-        nc.vector.tensor_copy(
-            out=q_grouped[:], in_=q_raw[:].unsqueeze(2).to_broadcast([P, B, Q_COPIES, PACK])
-        )
-        nc.vector.quantize_mx(
-            out=w_codes[:, W_C, :].bitcast(FP8X4),
-            scales=w_scales[:, W_C, :],
-            in_=w_grouped[:, W_C, :, :].rearrange("p h t -> p (h t)"),
-        )
-        q_codes = keep.tile([P, B * Q_COPIES], U32, align_bytes=64)
-        q_scales = keep.tile([P, B * Q_COPIES], U8, align_bytes=64)
-        nc.vector.quantize_mx(
-            out=q_codes[:].bitcast(FP8X4),
-            scales=q_scales[:],
-            in_=q_grouped[:].rearrange("p b s t -> p (b s t)"),
-        )
-        bias = keep.tile([P, 1], F32)
-        nc.vector.tensor_copy(out=bias[:], in_=bias_raw[:])
-        c_psum = fact_psum.tile([P, B, Q_COPIES], F32, tag="head")
-        mx_pass(c_psum[:].rearrange("p b s -> p (b s)"), W_C, q_codes[:], q_scales[:])
-        quantise_facts(1)
-        nc.vector.tensor_scalar(
-            out=c_sb[:], in0=c_psum[:, :, 0], scalar1=bias[:, 0:1], scalar2=None, op0=ADD
-        )
-        finish_v(0, v_psum_0)
-        finish_v(1, multiply_facts(1))
+        turn_facts(0)
+        spread_questions(0)
+        group_weights(FOR_U)
+        group_weights(FOR_V)
+        quantise_weights()
+        quantise_facts(0)
+        v_psum_0 = multiply(0)
 
         out_units = out.rearrange("b (g m r) h -> (b g) m r h", g=UNITS, m=P, r=RUN)
-        for unit in range(B * UNITS):
+        u_wide = keep.tile([P, B, T_BANK, J_UNIT, I_HI], F32)
+        v_wide = keep.tile([P, B, N, I_HI], F32)
+
+        def widen_u(b, copy):
+            copy(
+                out=u_wide[:, b, :, :, :],
+                in_=u_sb[:, b, T_BANK:RUN, :].unsqueeze(2).to_broadcast([P, T_BANK, J_UNIT, I_HI]),
+            )
+
+        def widen_v(b, first_unit):
+            j0 = first_unit * J_UNIT
+            nc.vector.tensor_copy(
+                out=v_wide[:, b, j0:N, :], in_=v_sb[:, b, j0:N].unsqueeze(2).to_broadcast([P, N - j0, I_HI])
+            )
+
+        def add(unit, r0, count):
             b, g = divmod(unit, UNITS)
-            pair_relu = pairs.tile([P, RUN, J_UNIT, I_HI], F32)
-            for j_lo in range(J_UNIT):
-                j = g * J_UNIT + j_lo
-                nc.vector.tensor_scalar(
-                    out=pair_relu[:, :, j_lo, :],
-                    in0=u_sb[:, b, :, :],
-                    scalar1=v_sb[:, b, j : j + 1],
-                    scalar2=0.0,
-                    op0=ADD,
-                    op1=MAX,
+            j0 = g * J_UNIT
+            shape = [P, count, J_UNIT, I_HI]
+            pair_sum = pairs.tile([P, T_BANK, J_UNIT, I_HI], F32)
+            v_part = (v_psum_0[:, b] if unit < RAMP else v_sb[:, b])[:, j0 : j0 + J_UNIT]
+            nc.vector.tensor_tensor(
+                out=pair_sum[:, 0:count, :, :],
+                in0=v_part.unsqueeze(1).unsqueeze(3).to_broadcast(shape),
+                in1=u_sb[:, b, r0 : r0 + count, :].unsqueeze(2).to_broadcast(shape),
+                op=ADD,
+            )
+            return pair_sum
+
+        def turn(pair_sum, count):
+            turned = turn_psum.tile([P, T_BANK, H], F32)
+            for r in range(count):
+                nc.tensor.transpose(
+                    turned[:, r, :], pair_sum[:, r, :, :].rearrange("p j i -> p (j i)"), identity[:]
                 )
-            stage = stages.tile([P, RUN, H], F32)
-            stored_at_once = T_BANK if unit == B * UNITS - 1 else RUN
-            for r0 in range(0, RUN, T_BANK):
-                turned = turn_psum.tile([P, T_BANK, H], F32)
-                for r in range(T_BANK):
-                    nc.tensor.transpose(
+            return turned
+
+        def turn_and_add(unit):
+            b, g = divmod(unit, UNITS)
+            j0 = g * J_UNIT
+            turned = turn_psum.tile([P, T_BANK, H], F32)
+            for r in range(T_BANK):
+                for first, part in (
+                    (True, u_wide[:, b, r, :, :]),
+                    (False, v_wide[:, b, j0 : j0 + J_UNIT, :]),
+                ):
+                    nc.tensor.matmul(
                         turned[:, r, :],
-                        pair_relu[:, r0 + r, :, :].rearrange("p j i -> p (j i)"),
+                        part.rearrange("p j i -> p (j i)"),
                         identity[:],
+                        start=first,
+                        stop=not first,
+                        is_transpose=True,
                     )
-                nc.scalar.copy(out=stage[:, r0 : r0 + T_BANK, :], in_=turned[:])
-                r_end = r0 + T_BANK
-                if r_end % stored_at_once == 0:
-                    nc.sync.dma_start(
-                        out=out_units[unit, :, r_end - stored_at_once : r_end, :],
-                        in_=stage[:, r_end - stored_at_once : r_end, :],
-                    )
+            return turned
+
+        def relu_out(stage, r0, count, turned, on_vector=False):
+            if on_vector:
+                nc.vector.tensor_scalar(
+                    out=stage[:, r0 : r0 + count, :], in0=turned[:, 0:count, :], scalar1=0.0, scalar2=None, op0=MAX
+                )
+            else:
+                nc.scalar.activation(out=stage[:, r0 : r0 + count, :], in_=turned[:, 0:count, :], func=RELU)
+
+        def store(unit, stage, r0, count):
+            nc.sync.dma_start(out=out_units[unit, :, r0 : r0 + count, :], in_=stage[:, r0 : r0 + count, :])
+
+        def adds(unit):
+            step = 2 if unit == 0 else T_BANK
+            return [add(unit, r0, step) for r0 in range(0, RUN if unit < RAMP else T_BANK, step)]
+
+        sums = adds(0)
+        for unit in range(B * UNITS):
+            next_sums = adds(unit + 1) if unit + 1 < B * UNITS else None
+            if unit == 0:
+                widen_u(0, nc.scalar.copy)
+                finish_v(0, v_psum_0)
+            if unit == 1:
+                widen_v(0, RAMP)
+            if unit % UNITS == UNITS - 1 and unit + 1 < B * UNITS:
+                widen_u(unit // UNITS + 1, nc.vector.tensor_copy)
+                widen_v(unit // UNITS + 1, 0)
+            stage = stages.tile([P, RUN, H], F32)
+            if unit == 0:
+                for r0 in range(0, RUN, 2):
+                    relu_out(stage, r0, 2, turn(sums[r0 // 2], 2))
+                    if r0 % T_BANK == 2:
+                        store(unit, stage, r0 - 2, T_BANK)
+            else:
+                relu_out(stage, 0, T_BANK, turn(sums[0], T_BANK), unit >= RAMP and unit % 2 == 1)
+                relu_out(stage, T_BANK, T_BANK, turn(sums[1], T_BANK) if unit < RAMP else turn_and_add(unit))
+                store(unit, stage, 0, RUN)
+            if unit == 2:
+                turn_facts(1)
+                spread_questions(1)
+            if unit == 3:
+                quantise_facts(1)
+            if unit == 4:
+                finish_v(1, multiply(1))
+            sums = next_sums

@@ -7,7 +7,6 @@ U32 = mybir.dt.uint32
 U8 = mybir.dt.uint8
 FP8X4 = mybir.dt.float8_e4m3fn_x4
 ADD = mybir.AluOpType.add
-MAX = mybir.AluOpType.max
 RELU = mybir.ActivationFunctionType.Relu
 IDENTITY = mybir.ActivationFunctionType.Identity
 
@@ -18,15 +17,15 @@ B = 4
 N = 64
 D = 256
 H = 128
-TILES = B * N // P
 B_TILE = P // N
+TILES = B // B_TILE
 HALF = D // PACK
 RUN = 8
 I_HI = N // RUN
 J_UNIT = P // I_HI
 UNITS = N // J_UNIT
 T_BANK = 4
-RAMP = 2
+PIECE = 2
 
 FOR_U = 0
 FOR_V = 1
@@ -41,7 +40,8 @@ def tile_relationnetwork_pa_t_kernel(tc, x, q, g_w0, g_b0, out):
         tc.tile_pool(name="pairs", bufs=4) as pairs,
         tc.tile_pool(name="stages", bufs=8) as stages,
         tc.psum_pool(name="head_psum", bufs=1) as head_psum,
-        tc.psum_pool(name="turn_psum", bufs=5) as turn_psum,
+        tc.psum_pool(name="v_psum", bufs=2) as v_psum_pool,
+        tc.psum_pool(name="turn_psum", bufs=4) as turn_psum,
         tc.manual_schedule(),
     ):
         x_twice = keep.tile([P, TILES, 2, D], BF16)
@@ -55,10 +55,10 @@ def tile_relationnetwork_pa_t_kernel(tc, x, q, g_w0, g_b0, out):
         w_quarters = g_w0.rearrange("(c p t) h -> c p t h", c=4, t=PACK)
         q_raw = keep.tile([P, B, PACK], BF16)
         bias = keep.tile([P, 1], BF16)
-        nc.scalar.dma_start(out=q_raw[:], in_=q.rearrange("b (p t) -> p b t", t=PACK))
-        load_facts(0)
         nc.sync.dma_start(out=w_raw[0:HALF, FOR_U, :, :], in_=w_quarters[0])
         nc.sync.dma_start(out=w_raw[HALF:P, FOR_U, :, :], in_=w_quarters[3])
+        load_facts(0)
+        nc.sync.dma_start(out=q_raw[:], in_=q.rearrange("b (p t) -> p b t", t=PACK))
         nc.sync.dma_start(out=w_raw[0:HALF, FOR_V, :, :], in_=w_quarters[2])
         nc.sync.dma_start(out=w_raw[HALF:P, FOR_V, :, :], in_=w_quarters[1])
         nc.sync.dma_start(out=bias[:], in_=g_b0.rearrange("(p o) -> p o", o=1))
@@ -67,9 +67,9 @@ def tile_relationnetwork_pa_t_kernel(tc, x, q, g_w0, g_b0, out):
         identity = keep.tile([P, P], F32)
         make_identity(nc, identity[:])
 
-        x_grouped = keep.tile([P, TILES, 2, P, PACK], BF16, align_bytes=64)
-        x_codes = keep.tile([P, TILES, 2, P], U32, align_bytes=64)
-        x_scales = keep.tile([P, TILES, 2, P], U8, align_bytes=64)
+        x_grouped = keep.tile([P, B, 2, N, PACK], BF16, align_bytes=64)
+        x_codes = keep.tile([P, B, 2, N], U32, align_bytes=64)
+        x_scales = keep.tile([P, B, 2, N], U8, align_bytes=64)
         w_grouped = keep.tile([P, 2, H, PACK], BF16, align_bytes=64)
         w_codes = keep.tile([P, 2, H], U32, align_bytes=64)
         w_scales = keep.tile([P, 2, H], U8, align_bytes=64)
@@ -83,102 +83,91 @@ def tile_relationnetwork_pa_t_kernel(tc, x, q, g_w0, g_b0, out):
             x_turned = head_psum.tile([P, 2, P], F32)
             for u in range(2):
                 nc.tensor.transpose(x_turned[:, u, :], pair_words[:, :, u], identity[:])
+            return x_turned
+
+        def group_facts(b, x_turned):
+            c0 = b % B_TILE * N
             for use, lo in ((FOR_U, 0), (FOR_V, HALF)):
                 nc.scalar.copy(
-                    out=words(x_grouped[lo : lo + HALF, a, use, :, :]).rearrange("p (c u) -> p c u", u=2),
-                    in_=x_turned[lo : lo + HALF, :, :].rearrange("p u c -> p c u"),
+                    out=words(x_grouped[lo : lo + HALF, b, use, :, :]).rearrange("p (c u) -> p c u", u=2),
+                    in_=x_turned[lo : lo + HALF, :, c0 : c0 + N].rearrange("p u c -> p c u"),
                 )
 
-        def quantise_facts(a):
+        def spread_question(b, use):
+            lo = 0 if use == FOR_V else HALF
+            nc.vector.tensor_copy(
+                out=words(x_grouped[lo : lo + HALF, b, use, :, :]).rearrange("p (n u) -> p n u", u=2),
+                in_=q_raw[lo : lo + HALF, b, :].bitcast(F32).unsqueeze(1).to_broadcast([HALF, N, 2]),
+            )
+
+        def quantise_facts(b, uses):
             nc.vector.quantize_mx(
-                out=x_codes[:, a, :, :].rearrange("p v c -> p (v c)").bitcast(FP8X4),
-                scales=x_scales[:, a, :, :].rearrange("p v c -> p (v c)"),
-                in_=x_grouped[:, a, :, :, :].rearrange("p v c t -> p (v c t)"),
+                out=x_codes[:, b, uses, :].rearrange("p v c -> p (v c)").bitcast(FP8X4),
+                scales=x_scales[:, b, uses, :].rearrange("p v c -> p (v c)"),
+                in_=x_grouped[:, b, uses, :, :].rearrange("p v c t -> p (v c t)"),
             )
 
         def group_weights(use):
             nc.vector.tensor_copy(out=w_grouped[:, use, :, :], in_=w_raw[:, use, :, :].rearrange("p t h -> p h t"))
 
-        def quantise_weights():
+        def quantise_weights(use):
             nc.vector.quantize_mx(
-                out=w_codes[:].rearrange("p v h -> p (v h)").bitcast(FP8X4),
-                scales=w_scales[:].rearrange("p v h -> p (v h)"),
-                in_=w_grouped[:].rearrange("p v h t -> p (v h t)"),
+                out=w_codes[:, use, :].bitcast(FP8X4),
+                scales=w_scales[:, use, :],
+                in_=w_grouped[:, use, :, :].rearrange("p h t -> p (h t)"),
             )
 
-        def spread_questions(a):
-            for use, lo in ((FOR_V, 0), (FOR_U, HALF)):
-                nc.vector.tensor_copy(
-                    out=words(x_grouped[lo : lo + HALF, a, use, :, :]).rearrange("p (s n u) -> p s n u", s=B_TILE, u=2),
-                    in_=words(q_raw[lo : lo + HALF, a * B_TILE : (a + 1) * B_TILE, :])
-                    .rearrange("p (s u) -> p s u", u=2)
-                    .unsqueeze(2)
-                    .to_broadcast([HALF, B_TILE, N, 2]),
-                )
-
         u_sb = keep.tile([P, B, RUN, I_HI], F32)
-        v_sb = keep.tile([P, B, N], F32)
 
-        def mx_pass(acc, a, use):
+        def mx_pass(acc, b, use):
             nc.tensor.matmul_mx(
                 out=acc,
                 lhsT=w_codes[:, use, :].bitcast(FP8X4),
                 lhsT_scale=w_scales[:, use, :],
-                rhs=x_codes[:, a, use, :].bitcast(FP8X4),
-                rhs_scale=x_scales[:, a, use, :],
+                rhs=x_codes[:, b, use, :].bitcast(FP8X4),
+                rhs_scale=x_scales[:, b, use, :],
                 start=True,
                 stop=True,
             )
 
-        def multiply(a):
-            u_psum = head_psum.tile([P, P], F32)
-            v_psum = head_psum.tile([P, B_TILE, N], F32)
-            mx_pass(u_psum[:], a, FOR_U)
-            mx_pass(v_psum[:].rearrange("p s j -> p (s j)"), a, FOR_V)
+        def multiply_u(b):
+            u_psum = head_psum.tile([P, N], F32)
+            mx_pass(u_psum[:], b, FOR_U)
             nc.scalar.activation(
-                out=u_sb[:, a * B_TILE : (a + 1) * B_TILE, :, :],
-                in_=u_psum[:].rearrange("p (s i r) -> p s r i", s=B_TILE, r=RUN),
+                out=u_sb[:, b, :, :],
+                in_=u_psum[:].rearrange("p (i r) -> p r i", r=RUN),
                 func=IDENTITY,
                 bias=bias[:, 0:1],
             )
+
+        def multiply_v(b):
+            v_psum = v_psum_pool.tile([P, N], F32)
+            mx_pass(v_psum[:], b, FOR_V)
             return v_psum
 
-        def finish_v(a, v_psum):
-            nc.vector.tensor_copy(out=v_sb[:, a * B_TILE : (a + 1) * B_TILE, :], in_=v_psum[:])
-
-        turn_facts(0)
-        spread_questions(0)
+        x_turned = turn_facts(0)
+        group_facts(0, x_turned)
         group_weights(FOR_U)
+        spread_question(0, FOR_U)
+        quantise_weights(FOR_U)
+        quantise_facts(0, slice(FOR_U, FOR_U + 1))
+        multiply_u(0)
         group_weights(FOR_V)
-        quantise_weights()
-        quantise_facts(0)
-        v_psum_0 = multiply(0)
+        spread_question(0, FOR_V)
+        quantise_weights(FOR_V)
+        quantise_facts(0, slice(FOR_V, FOR_V + 1))
+        v_psum = {0: multiply_v(0)}
 
         out_units = out.rearrange("b (g m r) h -> (b g) m r h", g=UNITS, m=P, r=RUN)
-        u_wide = keep.tile([P, B, T_BANK, J_UNIT, I_HI], F32)
-        v_wide = keep.tile([P, B, N, I_HI], F32)
-
-        def widen_u(b, copy):
-            copy(
-                out=u_wide[:, b, :, :, :],
-                in_=u_sb[:, b, T_BANK:RUN, :].unsqueeze(2).to_broadcast([P, T_BANK, J_UNIT, I_HI]),
-            )
-
-        def widen_v(b, first_unit):
-            j0 = first_unit * J_UNIT
-            nc.vector.tensor_copy(
-                out=v_wide[:, b, j0:N, :], in_=v_sb[:, b, j0:N].unsqueeze(2).to_broadcast([P, N - j0, I_HI])
-            )
 
         def add(unit, r0, count):
             b, g = divmod(unit, UNITS)
             j0 = g * J_UNIT
             shape = [P, count, J_UNIT, I_HI]
             pair_sum = pairs.tile([P, T_BANK, J_UNIT, I_HI], F32)
-            v_part = (v_psum_0[:, b] if unit < RAMP else v_sb[:, b])[:, j0 : j0 + J_UNIT]
             nc.vector.tensor_tensor(
                 out=pair_sum[:, 0:count, :, :],
-                in0=v_part.unsqueeze(1).unsqueeze(3).to_broadcast(shape),
+                in0=v_psum[b][:, j0 : j0 + J_UNIT].unsqueeze(1).unsqueeze(3).to_broadcast(shape),
                 in1=u_sb[:, b, r0 : r0 + count, :].unsqueeze(2).to_broadcast(shape),
                 op=ADD,
             )
@@ -192,66 +181,39 @@ def tile_relationnetwork_pa_t_kernel(tc, x, q, g_w0, g_b0, out):
                 )
             return turned
 
-        def turn_and_add(unit):
-            b, g = divmod(unit, UNITS)
-            j0 = g * J_UNIT
-            turned = turn_psum.tile([P, T_BANK, H], F32)
-            for r in range(T_BANK):
-                for first, part in (
-                    (True, u_wide[:, b, r, :, :]),
-                    (False, v_wide[:, b, j0 : j0 + J_UNIT, :]),
-                ):
-                    nc.tensor.matmul(
-                        turned[:, r, :],
-                        part.rearrange("p j i -> p (j i)"),
-                        identity[:],
-                        start=first,
-                        stop=not first,
-                        is_transpose=True,
-                    )
-            return turned
-
-        def relu_out(stage, r0, count, turned, on_vector=False):
-            if on_vector:
-                nc.vector.tensor_scalar(
-                    out=stage[:, r0 : r0 + count, :], in0=turned[:, 0:count, :], scalar1=0.0, scalar2=None, op0=MAX
-                )
-            else:
-                nc.scalar.activation(out=stage[:, r0 : r0 + count, :], in_=turned[:, 0:count, :], func=RELU)
+        def relu_out(stage, r0, count, turned):
+            nc.scalar.activation(out=stage[:, r0 : r0 + count, :], in_=turned[:, 0:count, :], func=RELU)
 
         def store(unit, stage, r0, count):
             nc.sync.dma_start(out=out_units[unit, :, r0 : r0 + count, :], in_=stage[:, r0 : r0 + count, :])
 
+        def rows_at_once(unit):
+            return PIECE if unit == 0 else T_BANK
+
         def adds(unit):
-            step = 2 if unit == 0 else T_BANK
-            return [add(unit, r0, step) for r0 in range(0, RUN if unit < RAMP else T_BANK, step)]
+            return [add(unit, r0, rows_at_once(unit)) for r0 in range(0, RUN, rows_at_once(unit))]
 
         sums = adds(0)
         for unit in range(B * UNITS):
+            next_b, g = unit // UNITS + 1, unit % UNITS
+            if next_b < B and g == 0:
+                if next_b % B_TILE == 0:
+                    x_turned = turn_facts(next_b // B_TILE)
+                group_facts(next_b, x_turned)
+                spread_question(next_b, FOR_U)
+                spread_question(next_b, FOR_V)
+            if next_b < B and g == 1:
+                multiply_u(next_b)
+                v_psum[next_b] = multiply_v(next_b)
             next_sums = adds(unit + 1) if unit + 1 < B * UNITS else None
-            if unit == 0:
-                widen_u(0, nc.scalar.copy)
-                finish_v(0, v_psum_0)
-            if unit == 1:
-                widen_v(0, RAMP)
-            if unit % UNITS == UNITS - 1 and unit + 1 < B * UNITS:
-                widen_u(unit // UNITS + 1, nc.vector.tensor_copy)
-                widen_v(unit // UNITS + 1, 0)
+            if next_b < B and g == 0:
+                quantise_facts(next_b, slice(FOR_U, FOR_V + 1))
             stage = stages.tile([P, RUN, H], F32)
-            if unit == 0:
-                for r0 in range(0, RUN, 2):
-                    relu_out(stage, r0, 2, turn(sums[r0 // 2], 2))
-                    if r0 % T_BANK == 2:
-                        store(unit, stage, r0 - 2, T_BANK)
-            else:
-                relu_out(stage, 0, T_BANK, turn(sums[0], T_BANK), unit >= RAMP and unit % 2 == 1)
-                relu_out(stage, T_BANK, T_BANK, turn(sums[1], T_BANK) if unit < RAMP else turn_and_add(unit))
+            count = rows_at_once(unit)
+            for k, pair_sum in enumerate(sums):
+                relu_out(stage, k * count, count, turn(pair_sum, count))
+                if unit == 0:
+                    store(unit, stage, k * count, count)
+            if unit > 0:
                 store(unit, stage, 0, RUN)
-            if unit == 2:
-                turn_facts(1)
-                spread_questions(1)
-            if unit == 3:
-                quantise_facts(1)
-            if unit == 4:
-                finish_v(1, multiply(1))
             sums = next_sums

@@ -7,6 +7,7 @@ U32 = mybir.dt.uint32
 U8 = mybir.dt.uint8
 FP8X4 = mybir.dt.float8_e4m3fn_x4
 ADD = mybir.AluOpType.add
+MAX = mybir.AluOpType.max
 RELU = mybir.ActivationFunctionType.Relu
 IDENTITY = mybir.ActivationFunctionType.Identity
 
@@ -29,6 +30,9 @@ PIECE = 2
 
 FOR_U = 0
 FOR_V = 1
+Q_COPIES = 16
+W_X = 0
+W_Q = 1
 
 FLOPS = 2 * B * N * N * (2 * D + K_PASS) * H
 
@@ -37,10 +41,10 @@ def tile_relationnetwork_pa_t_kernel(tc, x, q, g_w0, g_b0, out):
     nc = tc.nc
     with (
         tc.tile_pool(name="keep", bufs=1) as keep,
+        tc.tile_pool(name="pieces", bufs=4) as pieces,
         tc.tile_pool(name="pairs", bufs=4) as pairs,
         tc.tile_pool(name="stages", bufs=8) as stages,
         tc.psum_pool(name="head_psum", bufs=1) as head_psum,
-        tc.psum_pool(name="v_psum", bufs=2) as v_psum_pool,
         tc.psum_pool(name="turn_psum", bufs=4) as turn_psum,
         tc.manual_schedule(),
     ):
@@ -52,15 +56,14 @@ def tile_relationnetwork_pa_t_kernel(tc, x, q, g_w0, g_b0, out):
                 nc.sync.dma_start(out=x_twice[:, a, twin, :], in_=x_tiles[a])
 
         w_raw = keep.tile([P, 2, PACK, H], BF16)
-        w_quarters = g_w0.rearrange("(c p t) h -> c p t h", c=4, t=PACK)
-        q_raw = keep.tile([P, B, PACK], BF16)
+        w_halves = g_w0.rearrange("(c p t) h -> c p t h", c=2, t=PACK)
+        q_rows = keep.tile([P, K_PASS], BF16)
         bias = keep.tile([P, 1], BF16)
-        nc.sync.dma_start(out=w_raw[0:HALF, FOR_U, :, :], in_=w_quarters[0])
-        nc.sync.dma_start(out=w_raw[HALF:P, FOR_U, :, :], in_=w_quarters[3])
+        nc.vector.memset(q_rows[:].bitcast(F32), 0.0)
         load_facts(0)
-        nc.sync.dma_start(out=q_raw[:], in_=q.rearrange("b (p t) -> p b t", t=PACK))
-        nc.sync.dma_start(out=w_raw[0:HALF, FOR_V, :, :], in_=w_quarters[2])
-        nc.sync.dma_start(out=w_raw[HALF:P, FOR_V, :, :], in_=w_quarters[1])
+        nc.sync.dma_start(out=w_raw[:, W_X, :, :], in_=w_halves[W_X])
+        nc.sync.dma_start(out=q_rows[0:B, :], in_=q)
+        nc.sync.dma_start(out=w_raw[:, W_Q, :, :], in_=w_halves[W_Q])
         nc.sync.dma_start(out=bias[:], in_=g_b0.rearrange("(p o) -> p o", o=1))
         load_facts(1)
 
@@ -73,6 +76,12 @@ def tile_relationnetwork_pa_t_kernel(tc, x, q, g_w0, g_b0, out):
         w_grouped = keep.tile([P, 2, H, PACK], BF16, align_bytes=64)
         w_codes = keep.tile([P, 2, H], U32, align_bytes=64)
         w_scales = keep.tile([P, 2, H], U8, align_bytes=64)
+
+        q_grouped = keep.tile([P, B * Q_COPIES, PACK], BF16, align_bytes=64)
+        q_codes = keep.tile([P, B * Q_COPIES], U32, align_bytes=64)
+        q_scales = keep.tile([P, B * Q_COPIES], U8, align_bytes=64)
+        nc.vector.memset(x_grouped[HALF:P, :, FOR_U, :, :].rearrange("p b n t -> p b (n t)").bitcast(F32), 0.0)
+        nc.vector.memset(x_grouped[0:HALF, :, FOR_V, :, :].rearrange("p b n t -> p b (n t)").bitcast(F32), 0.0)
 
         def words(rows):
             return rows.rearrange("p c t -> p (c t)").bitcast(F32)
@@ -93,46 +102,68 @@ def tile_relationnetwork_pa_t_kernel(tc, x, q, g_w0, g_b0, out):
                     in_=x_turned[lo : lo + HALF, :, c0 : c0 + N].rearrange("p u c -> p c u"),
                 )
 
-        def spread_question(b, use):
-            lo = 0 if use == FOR_V else HALF
+        def turn_questions():
+            pair_words = q_rows[:].bitcast(F32).rearrange("r (p u) -> r p u", u=2)
+            q_turned = turn_psum.tile([P, T_BANK, H], F32, tag="turned")
+            for u in range(2):
+                nc.tensor.transpose(q_turned[:, u, :], pair_words[:, :, u], identity[:])
+            return q_turned
+
+        def group_questions(q_turned):
             nc.vector.tensor_copy(
-                out=words(x_grouped[lo : lo + HALF, b, use, :, :]).rearrange("p (n u) -> p n u", u=2),
-                in_=q_raw[lo : lo + HALF, b, :].bitcast(F32).unsqueeze(1).to_broadcast([HALF, N, 2]),
+                out=words(q_grouped[:]).rearrange("p (b n u) -> p b n u", b=B, u=2),
+                in_=q_turned[:, 0:2, 0:B].rearrange("p u b -> p b u").unsqueeze(2).to_broadcast([P, B, Q_COPIES, 2]),
             )
 
-        def quantise_facts(b, uses):
+        def quantise_questions():
             nc.vector.quantize_mx(
-                out=x_codes[:, b, uses, :].rearrange("p v c -> p (v c)").bitcast(FP8X4),
-                scales=x_scales[:, b, uses, :].rearrange("p v c -> p (v c)"),
-                in_=x_grouped[:, b, uses, :, :].rearrange("p v c t -> p (v c t)"),
+                out=q_codes[:].bitcast(FP8X4),
+                scales=q_scales[:],
+                in_=q_grouped[:].rearrange("p n t -> p (n t)"),
             )
 
-        def group_weights(use):
-            nc.vector.tensor_copy(out=w_grouped[:, use, :, :], in_=w_raw[:, use, :, :].rearrange("p t h -> p h t"))
-
-        def quantise_weights(use):
+        def quantise_facts(b):
             nc.vector.quantize_mx(
-                out=w_codes[:, use, :].bitcast(FP8X4),
-                scales=w_scales[:, use, :],
-                in_=w_grouped[:, use, :, :].rearrange("p h t -> p (h t)"),
+                out=x_codes[:, b, :, :].rearrange("p v c -> p (v c)").bitcast(FP8X4),
+                scales=x_scales[:, b, :, :].rearrange("p v c -> p (v c)"),
+                in_=x_grouped[:, b, :, :, :].rearrange("p v c t -> p (v c t)"),
+            )
+
+        def group_weights(half):
+            nc.vector.tensor_copy(out=w_grouped[:, half, :, :], in_=w_raw[:, half, :, :].rearrange("p t h -> p h t"))
+
+        def quantise_weights(half):
+            nc.vector.quantize_mx(
+                out=w_codes[:, half, :].bitcast(FP8X4),
+                scales=w_scales[:, half, :],
+                in_=w_grouped[:, half, :, :].rearrange("p h t -> p (h t)"),
             )
 
         u_sb = keep.tile([P, B, RUN, I_HI], F32)
+        v_sb = keep.tile([P, B, N], F32)
 
-        def mx_pass(acc, b, use):
+        def mx_pass(acc, half, codes, scales):
             nc.tensor.matmul_mx(
                 out=acc,
-                lhsT=w_codes[:, use, :].bitcast(FP8X4),
-                lhsT_scale=w_scales[:, use, :],
-                rhs=x_codes[:, b, use, :].bitcast(FP8X4),
-                rhs_scale=x_scales[:, b, use, :],
+                lhsT=w_codes[:, half, :].bitcast(FP8X4),
+                lhsT_scale=w_scales[:, half, :],
+                rhs=codes.bitcast(FP8X4),
+                rhs_scale=scales,
                 start=True,
                 stop=True,
             )
 
-        def multiply_u(b):
-            u_psum = head_psum.tile([P, N], F32)
-            mx_pass(u_psum[:], b, FOR_U)
+        def multiply(b, use):
+            acc = head_psum.tile([P, N], F32, tag="u_psum" if use == FOR_U else "v_psum")
+            mx_pass(acc[:], W_X, x_codes[:, b, use, :], x_scales[:, b, use, :])
+            return acc
+
+        def multiply_questions():
+            c_psum = head_psum.tile([P, B, Q_COPIES], F32)
+            mx_pass(c_psum[:].rearrange("p b n -> p (b n)"), W_Q, q_codes[:], q_scales[:])
+            return c_psum
+
+        def finish_u(b, u_psum):
             nc.scalar.activation(
                 out=u_sb[:, b, :, :],
                 in_=u_psum[:].rearrange("p (i r) -> p r i", r=RUN),
@@ -140,80 +171,96 @@ def tile_relationnetwork_pa_t_kernel(tc, x, q, g_w0, g_b0, out):
                 bias=bias[:, 0:1],
             )
 
-        def multiply_v(b):
-            v_psum = v_psum_pool.tile([P, N], F32)
-            mx_pass(v_psum[:], b, FOR_V)
-            return v_psum
+        def finish_v(b, v_psum):
+            nc.vector.tensor_scalar(
+                out=v_sb[:, b, :], in0=v_psum[:], scalar1=c_psum[:, b, 0:1], scalar2=None, op0=ADD
+            )
 
         x_turned = turn_facts(0)
         group_facts(0, x_turned)
-        group_weights(FOR_U)
-        spread_question(0, FOR_U)
-        quantise_weights(FOR_U)
-        quantise_facts(0, slice(FOR_U, FOR_U + 1))
-        multiply_u(0)
-        group_weights(FOR_V)
-        spread_question(0, FOR_V)
-        quantise_weights(FOR_V)
-        quantise_facts(0, slice(FOR_V, FOR_V + 1))
-        v_psum = {0: multiply_v(0)}
+        q_turned = turn_questions()
+        group_weights(W_X)
+        group_weights(W_Q)
+        quantise_weights(W_X)
+        group_questions(q_turned)
+        quantise_facts(0)
+        u_psum = multiply(0, FOR_U)
+        v_psum = multiply(0, FOR_V)
+        finish_u(0, u_psum)
+        quantise_weights(W_Q)
+        quantise_questions()
+        c_psum = multiply_questions()
+        finish_v(0, v_psum)
+        group_facts(1, x_turned)
+        x_turned = turn_facts(1)
+        group_facts(2, x_turned)
+        group_facts(3, x_turned)
 
         out_units = out.rearrange("b (g m r) h -> (b g) m r h", g=UNITS, m=P, r=RUN)
 
-        def add(unit, r0, count):
-            b, g = divmod(unit, UNITS)
-            j0 = g * J_UNIT
-            shape = [P, count, J_UNIT, I_HI]
-            pair_sum = pairs.tile([P, T_BANK, J_UNIT, I_HI], F32)
+        def add_piece(r0):
+            shape = [P, PIECE, J_UNIT, I_HI]
+            piece = pieces.tile([P, PIECE, J_UNIT, I_HI], F32)
             nc.vector.tensor_tensor(
-                out=pair_sum[:, 0:count, :, :],
-                in0=v_psum[b][:, j0 : j0 + J_UNIT].unsqueeze(1).unsqueeze(3).to_broadcast(shape),
-                in1=u_sb[:, b, r0 : r0 + count, :].unsqueeze(2).to_broadcast(shape),
+                out=piece[:],
+                in0=v_sb[:, 0, 0:J_UNIT].unsqueeze(1).unsqueeze(3).to_broadcast(shape),
+                in1=u_sb[:, 0, r0 : r0 + PIECE, :].unsqueeze(2).to_broadcast(shape),
                 op=ADD,
             )
-            return pair_sum
+            return piece
 
-        def turn(pair_sum, count):
+        def add_unit(unit):
+            b, g = divmod(unit, UNITS)
+            pair_relu = pairs.tile([P, RUN, J_UNIT, I_HI], F32)
+            for j_lo in range(J_UNIT):
+                j = g * J_UNIT + j_lo
+                nc.vector.tensor_scalar(
+                    out=pair_relu[:, :, j_lo, :],
+                    in0=u_sb[:, b, :, :],
+                    scalar1=v_sb[:, b, j : j + 1],
+                    scalar2=0.0,
+                    op0=ADD,
+                    op1=MAX,
+                )
+            return pair_relu
+
+        def turn(pairs_tile, r0, count):
             turned = turn_psum.tile([P, T_BANK, H], F32)
             for r in range(count):
                 nc.tensor.transpose(
-                    turned[:, r, :], pair_sum[:, r, :, :].rearrange("p j i -> p (j i)"), identity[:]
+                    turned[:, r, :], pairs_tile[:, r0 + r, :, :].rearrange("p j i -> p (j i)"), identity[:]
                 )
             return turned
-
-        def relu_out(stage, r0, count, turned):
-            nc.scalar.activation(out=stage[:, r0 : r0 + count, :], in_=turned[:, 0:count, :], func=RELU)
 
         def store(unit, stage, r0, count):
             nc.sync.dma_start(out=out_units[unit, :, r0 : r0 + count, :], in_=stage[:, r0 : r0 + count, :])
 
-        def rows_at_once(unit):
-            return PIECE if unit == 0 else T_BANK
-
-        def adds(unit):
-            return [add(unit, r0, rows_at_once(unit)) for r0 in range(0, RUN, rows_at_once(unit))]
-
-        sums = adds(0)
-        for unit in range(B * UNITS):
-            next_b, g = unit // UNITS + 1, unit % UNITS
-            if next_b < B and g == 0:
-                if next_b % B_TILE == 0:
-                    x_turned = turn_facts(next_b // B_TILE)
-                group_facts(next_b, x_turned)
-                spread_question(next_b, FOR_U)
-                spread_question(next_b, FOR_V)
-            if next_b < B and g == 1:
-                multiply_u(next_b)
-                v_psum[next_b] = multiply_v(next_b)
-            next_sums = adds(unit + 1) if unit + 1 < B * UNITS else None
-            if next_b < B and g == 0:
-                quantise_facts(next_b, slice(FOR_U, FOR_V + 1))
+        last = B * UNITS - 1
+        first_pieces = [add_piece(r0) for r0 in range(0, RUN, PIECE)]
+        ready = add_unit(1)
+        quantise_facts(1)
+        stage = stages.tile([P, RUN, H], F32)
+        for k, piece in enumerate(first_pieces):
+            turned = turn(piece, 0, PIECE)
+            nc.scalar.activation(out=stage[:, k * PIECE : (k + 1) * PIECE, :], in_=turned[:, 0:PIECE, :], func=RELU)
+            store(0, stage, k * PIECE, PIECE)
+        for unit in range(1, B * UNITS):
+            next_ready = add_unit(unit + 1) if unit < last else None
+            b, second = divmod(unit + 1, 2)
+            if b < B and second:
+                finish_v(b, v_psum)
+                if b + 1 < B:
+                    quantise_facts(b + 1)
             stage = stages.tile([P, RUN, H], F32)
-            count = rows_at_once(unit)
-            for k, pair_sum in enumerate(sums):
-                relu_out(stage, k * count, count, turn(pair_sum, count))
-                if unit == 0:
-                    store(unit, stage, k * count, count)
-            if unit > 0:
+            for r0 in range(0, RUN, T_BANK):
+                turned = turn(ready, r0, T_BANK)
+                nc.scalar.copy(out=stage[:, r0 : r0 + T_BANK, :], in_=turned[:])
+                if unit == last:
+                    store(unit, stage, r0, T_BANK)
+            if unit < last:
                 store(unit, stage, 0, RUN)
-            sums = next_sums
+            if b < B and not second:
+                u_psum = multiply(b, FOR_U)
+                v_psum = multiply(b, FOR_V)
+                finish_u(b, u_psum)
+            ready = next_ready

@@ -171,6 +171,17 @@ def tile_relationnetwork_pa_t_kernel(tc, x, q, g_w0, g_b0, out):
                 bias=bias[:, 0:1],
             )
 
+        v_first = keep.tile([P, J_UNIT, I_HI], F32)
+
+        def finish_v_first(v_psum):
+            nc.vector.tensor_scalar(
+                out=v_first[:],
+                in0=v_psum[:, 0:J_UNIT].unsqueeze(2).to_broadcast([P, J_UNIT, I_HI]),
+                scalar1=c_psum[:, 0, 0:1],
+                scalar2=None,
+                op0=ADD,
+            )
+
         def finish_v(b, v_psum):
             nc.vector.tensor_scalar(
                 out=v_sb[:, b, :], in0=v_psum[:], scalar1=c_psum[:, b, 0:1], scalar2=None, op0=ADD
@@ -190,7 +201,7 @@ def tile_relationnetwork_pa_t_kernel(tc, x, q, g_w0, g_b0, out):
         quantise_weights(W_Q)
         quantise_questions()
         c_psum = multiply_questions()
-        finish_v(0, v_psum)
+        finish_v_first(v_psum)
         group_facts(1, x_turned)
         x_turned = turn_facts(1)
         group_facts(2, x_turned)
@@ -203,7 +214,7 @@ def tile_relationnetwork_pa_t_kernel(tc, x, q, g_w0, g_b0, out):
             piece = pieces.tile([P, PIECE, J_UNIT, I_HI], F32)
             nc.vector.tensor_tensor(
                 out=piece[:],
-                in0=v_sb[:, 0, 0:J_UNIT].unsqueeze(1).unsqueeze(3).to_broadcast(shape),
+                in0=v_first[:].unsqueeze(1).to_broadcast(shape),
                 in1=u_sb[:, 0, r0 : r0 + PIECE, :].unsqueeze(2).to_broadcast(shape),
                 op=ADD,
             )
@@ -237,6 +248,7 @@ def tile_relationnetwork_pa_t_kernel(tc, x, q, g_w0, g_b0, out):
 
         last = B * UNITS - 1
         first_pieces = [add_piece(r0) for r0 in range(0, RUN, PIECE)]
+        finish_v(0, v_psum)
         ready = add_unit(1)
         quantise_facts(1)
         stage = stages.tile([P, RUN, H], F32)
@@ -255,9 +267,9 @@ def tile_relationnetwork_pa_t_kernel(tc, x, q, g_w0, g_b0, out):
             for r0 in range(0, RUN, T_BANK):
                 turned = turn(ready, r0, T_BANK)
                 nc.scalar.copy(out=stage[:, r0 : r0 + T_BANK, :], in_=turned[:])
-                if unit == last:
+                if unit in (1, last):
                     store(unit, stage, r0, T_BANK)
-            if unit < last:
+            if unit not in (1, last):
                 store(unit, stage, 0, RUN)
             if b < B and not second:
                 u_psum = multiply(b, FOR_U)

@@ -28,6 +28,7 @@ UNITS = N // J_UNIT
 T_BANK = 4
 PIECE = 2
 
+V_SHARE = 5
 FOR_U = 0
 FOR_V = 1
 Q_COPIES = 16
@@ -266,7 +267,10 @@ def tile_relationnetwork_pa_t_kernel(tc, x, q, g_w0, g_b0, out):
             stage = stages.tile([P, RUN, H], F32)
             for r0 in range(0, RUN, T_BANK):
                 turned = turn(ready, r0, T_BANK)
-                nc.scalar.copy(out=stage[:, r0 : r0 + T_BANK, :], in_=turned[:])
+                if r0 == 0 and unit % V_SHARE == V_SHARE - 1:
+                    nc.vector.tensor_copy(out=stage[:, r0 : r0 + T_BANK, :], in_=turned[:])
+                else:
+                    nc.scalar.copy(out=stage[:, r0 : r0 + T_BANK, :], in_=turned[:])
                 if unit in (1, last):
                     store(unit, stage, r0, T_BANK)
             if unit not in (1, last):

@@ -58,13 +58,12 @@ def tile_relationnetwork_pa_t_kernel(tc, x, q, g_w0, g_b0, out):
 
         w_raw = keep.tile([P, 2, PACK, H], BF16)
         w_halves = g_w0.rearrange("(c p t) h -> c p t h", c=2, t=PACK)
-        q_rows = keep.tile([P, K_PASS], BF16)
+        q_raw = keep.tile([P, B, PACK], BF16)
         bias = keep.tile([P, 1], BF16)
-        nc.vector.memset(q_rows[:].bitcast(F32), 0.0)
         load_facts(0)
         nc.sync.dma_start(out=w_raw[:, W_X, :, :], in_=w_halves[W_X])
-        nc.sync.dma_start(out=q_rows[0:B, :], in_=q)
         nc.sync.dma_start(out=w_raw[:, W_Q, :, :], in_=w_halves[W_Q])
+        nc.sync.dma_start(out=q_raw[:], in_=q.rearrange("b (p t) -> p b t", t=PACK))
         nc.sync.dma_start(out=bias[:], in_=g_b0.rearrange("(p o) -> p o", o=1))
         load_facts(1)
 
@@ -103,17 +102,10 @@ def tile_relationnetwork_pa_t_kernel(tc, x, q, g_w0, g_b0, out):
                     in_=x_turned[lo : lo + HALF, :, c0 : c0 + N].rearrange("p u c -> p c u"),
                 )
 
-        def turn_questions():
-            pair_words = q_rows[:].bitcast(F32).rearrange("r (p u) -> r p u", u=2)
-            q_turned = turn_psum.tile([P, T_BANK, H], F32, tag="turned")
-            for u in range(2):
-                nc.tensor.transpose(q_turned[:, u, :], pair_words[:, :, u], identity[:])
-            return q_turned
-
-        def group_questions(q_turned):
+        def group_questions():
             nc.vector.tensor_copy(
-                out=words(q_grouped[:]).rearrange("p (b n u) -> p b n u", b=B, u=2),
-                in_=q_turned[:, 0:2, 0:B].rearrange("p u b -> p b u").unsqueeze(2).to_broadcast([P, B, Q_COPIES, 2]),
+                out=q_grouped[:].rearrange("p (b n) t -> p b n t", b=B),
+                in_=q_raw[:].unsqueeze(2).to_broadcast([P, B, Q_COPIES, PACK]),
             )
 
         def quantise_questions():
@@ -190,12 +182,11 @@ def tile_relationnetwork_pa_t_kernel(tc, x, q, g_w0, g_b0, out):
 
         x_turned = turn_facts(0)
         group_facts(0, x_turned)
-        q_turned = turn_questions()
         group_weights(W_X)
-        group_weights(W_Q)
         quantise_weights(W_X)
-        group_questions(q_turned)
+        group_weights(W_Q)
         quantise_facts(0)
+        group_questions()
         u_psum = multiply(0, FOR_U)
         v_psum = multiply(0, FOR_V)
         finish_u(0, u_psum)
@@ -204,9 +195,6 @@ def tile_relationnetwork_pa_t_kernel(tc, x, q, g_w0, g_b0, out):
         c_psum = multiply_questions()
         finish_v_first(v_psum)
         group_facts(1, x_turned)
-        x_turned = turn_facts(1)
-        group_facts(2, x_turned)
-        group_facts(3, x_turned)
 
         out_units = out.rearrange("b (g m r) h -> (b g) m r h", g=UNITS, m=P, r=RUN)
 
@@ -257,6 +245,9 @@ def tile_relationnetwork_pa_t_kernel(tc, x, q, g_w0, g_b0, out):
             turned = turn(piece, 0, PIECE)
             nc.scalar.activation(out=stage[:, k * PIECE : (k + 1) * PIECE, :], in_=turned[:, 0:PIECE, :], func=RELU)
             store(0, stage, k * PIECE, PIECE)
+        x_turned = turn_facts(1)
+        group_facts(2, x_turned)
+        group_facts(3, x_turned)
         for unit in range(1, B * UNITS):
             next_ready = add_unit(unit + 1) if unit < last else None
             b, second = divmod(unit + 1, 2)

import concourse.mybir as mybir
from concourse.masks import make_identity

F32 = mybir.dt.float32
BF16 = mybir.dt.bfloat16
U32 = mybir.dt.uint32
U8 = mybir.dt.uint8
FP8X4 = mybir.dt.float8_e4m3fn_x4
ADD = mybir.AluOpType.add
MAX = mybir.AluOpType.max
RELU = mybir.ActivationFunctionType.Relu
IDENTITY = mybir.ActivationFunctionType.Identity

P = 128
PACK = 4
K_PASS = P * PACK
B = 4
N = 64
D = 256
H = 128
B_TILE = P // N
TILES = B // B_TILE
HALF = D // PACK
RUN = 8
I_HI = N // RUN
J_UNIT = P // I_HI
UNITS = N // J_UNIT
T_BANK = 4
PIECE = 2

V_SHARE = 5
FOR_U = 0
FOR_V = 1
Q_COPIES = 16
W_X = 0
W_Q = 1

FLOPS = 2 * B * N * N * (2 * D + K_PASS) * H


def tile_relationnetwork_pa_t_kernel(tc, x, q, g_w0, g_b0, out):
    nc = tc.nc
    with (
        tc.tile_pool(name="keep", bufs=1) as keep,
        tc.tile_pool(name="pieces", bufs=4) as pieces,
        tc.tile_pool(name="pairs", bufs=4) as pairs,
        tc.tile_pool(name="stages", bufs=8) as stages,
        tc.psum_pool(name="head_psum", bufs=1) as head_psum,
        tc.psum_pool(name="turn_psum", bufs=4) as turn_psum,
        tc.manual_schedule(),
    ):
        x_twice = keep.tile([P, TILES, 2, D], BF16)
        x_tiles = x.rearrange("b n k -> (b n) k").rearrange("(a r) k -> a r k", r=P)

        def load_facts(a):
            for twin in range(2):
                nc.sync.dma_start(out=x_twice[:, a, twin, :], in_=x_tiles[a])

        w_raw = keep.tile([P, 2, PACK, H], BF16)
        w_halves = g_w0.rearrange("(c p t) h -> c p t h", c=2, t=PACK)
        q_raw = keep.tile([P, B, PACK], BF16)
        bias = keep.tile([P, 1], BF16)
        load_facts(0)
        nc.sync.dma_start(out=w_raw[:, W_X, :, :], in_=w_halves[W_X])
        nc.sync.dma_start(out=w_raw[:, W_Q, :, :], in_=w_halves[W_Q])
        nc.sync.dma_start(out=q_raw[:], in_=q.rearrange("b (p t) -> p b t", t=PACK))
        nc.sync.dma_start(out=bias[:], in_=g_b0.rearrange("(p o) -> p o", o=1))
        load_facts(1)

        identity = keep.tile([P, P], F32)
        make_identity(nc, identity[:])

        x_grouped = keep.tile([P, B, 2, N, PACK], BF16, align_bytes=64)
        x_codes = keep.tile([P, B, 2, N], U32, align_bytes=64)
        x_scales = keep.tile([P, B, 2, N], U8, align_bytes=64)
        w_grouped = keep.tile([P, 2, H, PACK], BF16, align_bytes=64)
        w_codes = keep.tile([P, 2, H], U32, align_bytes=64)
        w_scales = keep.tile([P, 2, H], U8, align_bytes=64)

        q_grouped = keep.tile([P, B * Q_COPIES, PACK], BF16, align_bytes=64)
        q_codes = keep.tile([P, B * Q_COPIES], U32, align_bytes=64)
        q_scales = keep.tile([P, B * Q_COPIES], U8, align_bytes=64)
        nc.vector.memset(x_grouped[HALF:P, :, FOR_U, :, :].rearrange("p b n t -> p b (n t)").bitcast(F32), 0.0)
        nc.vector.memset(x_grouped[0:HALF, :, FOR_V, :, :].rearrange("p b n t -> p b (n t)").bitcast(F32), 0.0)

        def words(rows):
            return rows.rearrange("p c t -> p (c t)").bitcast(F32)

        def turn_facts(a):
            pair_words = x_twice[:, a, :, :].rearrange("r d k -> r (d k)").bitcast(F32)
            pair_words = pair_words.rearrange("r (p u) -> r p u", u=2)
            x_turned = head_psum.tile([P, 2, P], F32)
            for u in range(2):
                nc.tensor.transpose(x_turned[:, u, :], pair_words[:, :, u], identity[:])
            return x_turned

        def group_facts(b, x_turned):
            c0 = b % B_TILE * N
            for use, lo in ((FOR_U, 0), (FOR_V, HALF)):
                nc.scalar.copy(
                    out=words(x_grouped[lo : lo + HALF, b, use, :, :]).rearrange("p (c u) -> p c u", u=2),
                    in_=x_turned[lo : lo + HALF, :, c0 : c0 + N].rearrange("p u c -> p c u"),
                )

        def group_questions():
            nc.vector.tensor_copy(
                out=q_grouped[:].rearrange("p (b n) t -> p b n t", b=B),
                in_=q_raw[:].unsqueeze(2).to_broadcast([P, B, Q_COPIES, PACK]),
            )

        def quantise_questions():
            nc.vector.quantize_mx(
                out=q_codes[:].bitcast(FP8X4),
                scales=q_scales[:],
                in_=q_grouped[:].rearrange("p n t -> p (n t)"),
            )

        def quantise_facts(b):
            nc.vector.quantize_mx(
                out=x_codes[:, b, :, :].rearrange("p v c -> p (v c)").bitcast(FP8X4),
                scales=x_scales[:, b, :, :].rearrange("p v c -> p (v c)"),
                in_=x_grouped[:, b, :, :, :].rearrange("p v c t -> p (v c t)"),
            )

        def group_weights(half):
            nc.vector.tensor_copy(out=w_grouped[:, half, :, :], in_=w_raw[:, half, :, :].rearrange("p t h -> p h t"))

        def quantise_weights(half):
            nc.vector.quantize_mx(
                out=w_codes[:, half, :].bitcast(FP8X4),
                scales=w_scales[:, half, :],
                in_=w_grouped[:, half, :, :].rearrange("p h t -> p (h t)"),
            )

        u_sb = keep.tile([P, B, RUN, I_HI], F32)
        v_sb = keep.tile([P, B, N], F32)

        def mx_pass(acc, half, codes, scales):
            nc.tensor.matmul_mx(
                out=acc,
                lhsT=w_codes[:, half, :].bitcast(FP8X4),
                lhsT_scale=w_scales[:, half, :],
                rhs=codes.bitcast(FP8X4),
                rhs_scale=scales,
                start=True,
                stop=True,
            )

        def multiply(b, use):
            acc = head_psum.tile([P, N], F32, tag="u_psum" if use == FOR_U else "v_psum")
            mx_pass(acc[:], W_X, x_codes[:, b, use, :], x_scales[:, b, use, :])
            return acc

        def multiply_questions():
            c_psum = head_psum.tile([P, B, Q_COPIES], F32)
            mx_pass(c_psum[:].rearrange("p b n -> p (b n)"), W_Q, q_codes[:], q_scales[:])
            return c_psum

        def finish_u(b, u_psum):
            nc.scalar.activation(
                out=u_sb[:, b, :, :],
                in_=u_psum[:].rearrange("p (i r) -> p r i", r=RUN),
                func=IDENTITY,
                bias=bias[:, 0:1],
            )

        v_first = keep.tile([P, J_UNIT, I_HI], F32)

        def finish_v_first(v_psum):
            nc.vector.tensor_scalar(
                out=v_first[:],
                in0=v_psum[:, 0:J_UNIT].unsqueeze(2).to_broadcast([P, J_UNIT, I_HI]),
                scalar1=c_psum[:, 0, 0:1],
                scalar2=None,
                op0=ADD,
            )

        def finish_v(b, v_psum):
            nc.vector.tensor_scalar(
                out=v_sb[:, b, :], in0=v_psum[:], scalar1=c_psum[:, b, 0:1], scalar2=None, op0=ADD
            )

        x_turned = turn_facts(0)
        group_facts(0, x_turned)
        group_weights(W_X)
        quantise_weights(W_X)
        group_weights(W_Q)
        quantise_facts(0)
        group_questions()
        u_psum = multiply(0, FOR_U)
        v_psum = multiply(0, FOR_V)
        finish_u(0, u_psum)
        quantise_weights(W_Q)
        quantise_questions()
        c_psum = multiply_questions()
        finish_v_first(v_psum)
        group_facts(1, x_turned)

        out_units = out.rearrange("b (g m r) h -> (b g) m r h", g=UNITS, m=P, r=RUN)

        def add_piece(r0):
            shape = [P, PIECE, J_UNIT, I_HI]
            piece = pieces.tile([P, PIECE, J_UNIT, I_HI], F32)
            nc.vector.tensor_tensor(
                out=piece[:],
                in0=v_first[:].unsqueeze(1).to_broadcast(shape),
                in1=u_sb[:, 0, r0 : r0 + PIECE, :].unsqueeze(2).to_broadcast(shape),
                op=ADD,
            )
            return piece

        def add_unit(unit):
            b, g = divmod(unit, UNITS)
            pair_relu = pairs.tile([P, RUN, J_UNIT, I_HI], F32)
            for j_lo in range(J_UNIT):
                j = g * J_UNIT + j_lo
                nc.vector.tensor_scalar(
                    out=pair_relu[:, :, j_lo, :],
                    in0=u_sb[:, b, :, :],
                    scalar1=v_sb[:, b, j : j + 1],
                    scalar2=0.0,
                    op0=ADD,
                    op1=MAX,
                )
            return pair_relu

        def turn(pairs_tile, r0, count):
            turned = turn_psum.tile([P, T_BANK, H], F32)
            for r in range(count):
                nc.tensor.transpose(
                    turned[:, r, :], pairs_tile[:, r0 + r, :, :].rearrange("p j i -> p (j i)"), identity[:]
                )
            return turned

        def store(unit, stage, r0, count):
            nc.sync.dma_start(out=out_units[unit, :, r0 : r0 + count, :], in_=stage[:, r0 : r0 + count, :])

        last = B * UNITS - 1
        first_pieces = [add_piece(r0) for r0 in range(0, RUN, PIECE)]
        finish_v(0, v_psum)
        ready = add_unit(1)
        quantise_facts(1)
        stage = stages.tile([P, RUN, H], F32)
        for k, piece in enumerate(first_pieces):
            turned = turn(piece, 0, PIECE)
            nc.scalar.activation(out=stage[:, k * PIECE : (k + 1) * PIECE, :], in_=turned[:, 0:PIECE, :], func=RELU)
            store(0, stage, k * PIECE, PIECE)
        x_turned = turn_facts(1)
        group_facts(2, x_turned)
        group_facts(3, x_turned)
        for unit in range(1, B * UNITS):
            next_ready = add_unit(unit + 1) if unit < last else None
            b, second = divmod(unit + 1, 2)
            if b < B and second:
                finish_v(b, v_psum)
                if b + 1 < B:
                    quantise_facts(b + 1)
            stage = stages.tile([P, RUN, H], F32)
            for r0 in range(0, RUN, T_BANK):
                turned = turn(ready, r0, T_BANK)
                if r0 == 0 and unit % V_SHARE == V_SHARE - 1:
                    nc.vector.tensor_copy(out=stage[:, r0 : r0 + T_BANK, :], in_=turned[:])
                else:
                    nc.scalar.copy(out=stage[:, r0 : r0 + T_BANK, :], in_=turned[:])
                if unit in (1, last):
                    store(unit, stage, r0, T_BANK)
            if unit not in (1, last):
                store(unit, stage, 0, RUN)
            if b < B and not second:
                u_psum = multiply(b, FOR_U)
                v_psum = multiply(b, FOR_V)
                finish_u(b, u_psum)
            ready = next_ready
